import numpy as np
import ml_dtypes


def mxq(x, axis, fmt="e4m3"):
    dtype, down = {"e4m3": (ml_dtypes.float8_e4m3fn, 7), "e5m2": (ml_dtypes.float8_e5m2, 14)}[fmt]
    v = np.moveaxis(np.asarray(x, np.float32).astype(ml_dtypes.bfloat16).astype(np.float64), axis, -1)
    blocks = v.reshape(v.shape[:-1] + (-1, 32))
    amax = np.abs(blocks).max(-1, keepdims=True)
    byte = np.maximum(np.where(amax > 0, np.frexp(amax)[1] - 1 + 127, 0) - down, 1)
    scale = np.exp2(byte - 127.0)
    codes = (blocks / scale).astype(np.float32).astype(dtype).astype(np.float64)
    return np.moveaxis((codes * scale).reshape(v.shape), -1, axis)


WIDE = False


def mx_kscale(k):
    if not WIDE:
        return np.ones(k)
    levels = np.array([10, -10, 5, -5, 0])
    a = np.random.permutation(np.resize(levels, k // 512 * 4)).reshape(k // 512, 4)
    idx = np.arange(k)
    return np.exp2(a[idx // 512, idx % 128 // 32])


BF16 = ml_dtypes.bfloat16


def bf(x):
    return np.asarray(x, np.float32).astype(BF16)


def f64(x):
    return np.asarray(x).astype(np.float64)


B, C, H, W, T, HID = 128, 2048, 3, 4, 20, 1024
S = H * W


def softmax_pos(h):
    e = np.exp(h - h.max(axis=1, keepdims=True))
    return e / e.sum(axis=1, keepdims=True)


def setup_inputs():
    s = mx_kscale(C)
    return {"v_i": bf(np.random.standard_normal((B, C, H, W)) * s[None, :, None, None]),
            "v_q": bf(np.random.standard_normal((B, T, HID))),
            "l1_w": bf(np.random.standard_normal((HID, C)) / np.sqrt(C) / s[None, :]),
            "l1_b": bf(np.random.standard_normal(HID) * 0.1),
            "w_vi0": bf(np.random.standard_normal((HID, HID)) * 1.5 / np.sqrt(HID)),
            "w_u0": bf(np.random.standard_normal((HID, HID)) * 2.0 / np.sqrt(HID)),
            "b_u0": bf(np.random.standard_normal(HID) * 0.5)}


def reference(v_i, v_q, l1_w, l1_b, w_vi0, w_u0, b_u0):
    x = f64(v_i).reshape(B, C, S).transpose(0, 2, 1)
    vi = np.tanh((mxq(x, 2, "e4m3") @ mxq(f64(l1_w).T, 0, "e4m3")) + f64(l1_b))
    u = f64(v_q).mean(axis=1)
    v_i_t = mxq(vi, 2, "e4m3") @ mxq(f64(w_vi0).T, 0, "e4m3")
    v_q_t = (mxq(u, 1, "e4m3") @ mxq(f64(w_u0).T, 0, "e4m3")) + f64(b_u0)
    h_a = np.tanh(v_i_t + v_q_t[:, None, :])
    p_i = softmax_pos(h_a)
    return u + (p_i * vi).sum(axis=1)

@@ -1,0 +1,452 @@
+from contextlib import ExitStack
+
+import concourse.masks as masks
+import concourse.mybir as mybir
+
+F32 = mybir.dt.float32
+BF16 = mybir.dt.bfloat16
+U32 = mybir.dt.uint32
+U8 = mybir.dt.uint8
+FP8X4 = mybir.dt.float8_e4m3fn_x4
+ACT = mybir.ActivationFunctionType
+ALU = mybir.AluOpType
+AX = mybir.AxisListType
+
+P = 128
+B, C, S, T, HID = 128, 2048, 12, 20, 1024
+FLOPS = 2 * B * S * HID * C + 2 * B * S * HID * HID + 2 * B * HID * HID
+
+NJ = 4
+BJ = B // NJ
+COLS = BJ * S
+SPLIT = ((0, 256), (256, 128))
+
+
+LAG_QW = 2
+LAG_QX = 1
+LAG_CAST = 1
+LAG_QV = 3
+LAG_TE = 2
+LAG_PROD = 4
+LAG_NUM = 1
+PRE = 2
+Q = 2
+
+
+def tile_attentionmechanism_pa_kernel(tc, v_i, v_q, l1_w, l1_b, w_vi0, w_u0, b_u0, out):
+    nc = tc.nc
+    with ExitStack() as ctx:
+        ctx.enter_context(tc.manual_schedule())
+        const = ctx.enter_context(tc.tile_pool(name="const", bufs=1))
+        ldw = ctx.enter_context(tc.tile_pool(name="ldw", bufs=4))
+        b6 = ctx.enter_context(tc.tile_pool(name="b6", bufs=8))
+        a12 = ctx.enter_context(tc.tile_pool(name="a12", bufs=3))
+        gwp = ctx.enter_context(tc.tile_pool(name="gwp", bufs=4))
+        vwp = ctx.enter_context(tc.tile_pool(name="vwp", bufs=3))
+        small = ctx.enter_context(tc.tile_pool(name="small", bufs=2))
+        psum = ctx.enter_context(tc.psum_pool(name="psum", bufs=8))
+
+        ident_f = const.tile([P, P], F32, name="ident_f")
+        masks.make_identity(nc, ident_f[:])
+        ident_b = const.tile([P, P], BF16, name="ident_b")
+        masks.make_identity(nc, ident_b[:])
+
+        lb_raw = const.tile([P, 8], BF16, name="lb_raw")
+        bu_raw = const.tile([P, 8], BF16, name="bu_raw")
+        nc.scalar.dma_start(out=lb_raw[:].rearrange("p (a e) -> p a e", e=2),
+                            in_=l1_b.rearrange("(a p e) -> p a e", p=P, e=2))
+        nc.scalar.dma_start(out=bu_raw[:].rearrange("p (a e) -> p a e", e=2),
+                            in_=b_u0.rearrange("(a p e) -> p a e", p=P, e=2))
+        lb = const.tile([P, 8], F32, name="lb")
+        bu = const.tile([P, 8], F32, name="bu")
+
+        words = {"l1": const.tile([P, 4, HID], U32, name="l1w", align_bytes=64),
+                 "wv": const.tile([P, 2, HID], U32, name="wvw", align_bytes=64),
+                 "wu": const.tile([P, 2, HID], U32, name="wuw", align_bytes=64)}
+        planes = {"l1": const.tile([P, 4, HID], U8, name="l1s", align_bytes=64),
+                  "wv": const.tile([P, 2, HID], U8, name="wvs", align_bytes=64),
+                  "wu": const.tile([P, 2, HID], U8, name="wus", align_bytes=64)}
+        xw = const.tile([P, 4, B * S], U32, name="xw", align_bytes=64)
+        xs = const.tile([P, 4, B * S], U8, name="xs", align_bytes=64)
+        uw = const.tile([P, 2 * B], U32, name="uw", align_bytes=64)
+        us = const.tile([P, 2 * B], U8, name="us", align_bytes=64)
+        u_sb = const.tile([P, HID], F32, name="u_sb")
+        vqt = const.tile([P, 8, B], F32, name="vqt")
+        res = const.tile([P, 8, B], F32, name="res")
+        osb = const.tile([P, HID], F32, name="osb")
+
+        t = {}
+
+        l1_rows = l1_w.rearrange("(a p e) c -> a p e c", p=P, e=2)
+        x_flat = v_i.rearrange("b c h w -> b (c h w)")
+        w_rows = {"wu": w_u0.rearrange("(k a p e) c -> k p a e c", a=2, p=P, e=2),
+                  "wv": w_vi0.rearrange("(k a p e) c -> k p a e c", a=2, p=P, e=2)}
+
+        def ld(what, i):
+            if what == "l1":
+                t["l1", i] = ldw.tile([P, 2, C], BF16, tag="ldw", name="l1sb")
+                nc.sync.dma_start(out=t["l1", i][:], in_=l1_rows[i])
+            elif what == "x":
+                t["x", i] = b6.tile([P, 256 * S], BF16, tag="b6", name="xq", align_bytes=64)
+                nc.sync.dma_start(out=t["x", i][:], in_=x_flat[:, 256 * S * i:256 * S * (i + 1)])
+            elif what == "vq":
+                nt = min(3, T - 3 * i)
+                t["vq", i] = b6.tile([P, 3, HID], BF16, tag="b6", name="vq", align_bytes=64)
+                nc.sync.dma_start(out=t["vq", i][:, 0:nt, :], in_=v_q[:, 3 * i:3 * i + nt, :])
+            else:
+                t[what, i] = ldw.tile([P, 2, 2, HID], BF16, tag="ldw", name="wsb")
+                nc.sync.dma_start(out=t[what, i][:], in_=w_rows[what][i])
+
+        def rows_of(w, a, e):
+            if w == "l1":
+                return t["l1", a][:, e, :]
+            return t[w, a // 2][:, a % 2, e, :]
+
+        def copy_on(eng, dst, src):
+            if eng == "V":
+                nc.vector.tensor_copy(out=dst, in_=src)
+            else:
+                nc.scalar.copy(out=dst, in_=src)
+
+        def tw(w, a, g):
+            bank = psum.tile([P, 2, 2, P], F32, tag="ps", name="wbank")
+            t["wb", w, a, g] = bank
+            for u in range(2):
+                for e in range(2):
+                    nc.tensor.transpose(
+                        bank[:, u, e, :],
+                        rows_of(w, a, e).bitcast(F32)[:, 256 * g + 128 * u:256 * g + 128 * u + 128],
+                        ident_f[:])
+
+        def ew(w, a, g, eng):
+            gw = gwp.tile([P, 1024], BF16, tag="gw", name="gw", align_bytes=64)
+            t["gw", w, a, g] = gw
+            copy_on(eng, gw[:].bitcast(F32).rearrange("p (c u) -> p c u", u=2),
+                    t["wb", w, a, g][:].rearrange("p u e h -> p (e h) u"))
+
+        def qw(w, a, g):
+            nc.vector.quantize_mx(out=words[w][:, g, 256 * a:256 * a + 256].bitcast(FP8X4),
+                                  scales=planes[w][:, g, 256 * a:256 * a + 256],
+                                  in_=t["gw", w, a, g][:])
+
+        def tx(g, i):
+            bank = psum.tile([P, 4, P], F32, tag="ps", name="xbank")
+            t["xb", g, i] = bank
+            for u in range(2):
+                xv = t["x", 2 * g + u][:].bitcast(F32).rearrange("b (p e i) -> b e i p", p=P, e=2, i=6)
+                for e in range(2):
+                    nc.tensor.transpose(bank[:, 2 * u + e, :], xv[:, e, i, :], ident_f[:])
+
+        def ex(g, i, eng):
+            if ("gx", g) not in t:
+                t["gx", g] = a12.tile([P, B * S * 4], BF16, tag="a12", name="gx", align_bytes=64)
+            gxv = t["gx", g][:].rearrange("p (b i r t) -> p i b r t", b=B, i=6, r=2, t=4)
+            copy_on(eng, gxv[:, i], t["xb", g, i][:].bitcast(BF16).rearrange("p t (b r) -> p b r t", r=2))
+
+        def qx(g, k):
+            nc.vector.quantize_mx(out=xw[:, g, 512 * k:512 * k + 512].bitcast(FP8X4),
+                                  scales=xs[:, g, 512 * k:512 * k + 512],
+                                  in_=t["gx", g][:, 2048 * k:2048 * k + 2048])
+
+        def m1(j, m):
+            ps = psum.tile([P, COLS], F32, tag="ps", name="ps1")
+            t["p1", j, m] = ps
+            for c0, n in SPLIT:
+                for g in range(4):
+                    nc.tensor.matmul_mx(
+                        out=ps[:, c0:c0 + n],
+                        lhsT=words["l1"][:, g, P * m:P * m + P].bitcast(FP8X4),
+                        lhsT_scale=planes["l1"][:, g, P * m:P * m + P],
+                        rhs=xw[:, g, COLS * j + c0:COLS * j + c0 + n].bitcast(FP8X4),
+                        rhs_scale=xs[:, g, COLS * j + c0:COLS * j + c0 + n],
+                        start=(g == 0), stop=(g == 3))
+
+        def th1(j, m):
+            if m == 0:
+                t["vi", j] = a12.tile([P, 8, COLS], F32, tag="a12", name="vi", align_bytes=64)
+            nc.scalar.activation(out=t["vi", j][:, m, :], in_=t["p1", j, m][:], func=ACT.Tanh,
+                                 bias=lb[:, m:m + 1], scale=1.0)
+
+        def cast(j, gp, eng):
+            if gp == 0:
+                t["gv", j] = b6.tile([P, 2, COLS * 4], BF16, tag="b6", name="gv", align_bytes=64)
+            dst = t["gv", j][:, gp, :].rearrange("p (c t) -> p c t", t=4)
+            src = t["vi", j][:, 4 * gp:4 * gp + 4, :].rearrange("p t c -> p c t")
+            if eng == "V":
+                nc.vector.tensor_copy(out=dst, in_=src)
+            else:
+                nc.gpsimd.tensor_scalar(out=dst, in0=src, scalar1=1.0, scalar2=0.0,
+                                        op0=ALU.mult, op1=ALU.add)
+
+        def qv(j, gp):
+            if gp == 0:
+                t["viw", j] = vwp.tile([P, 2, COLS], U32, tag="viw", name="viw", align_bytes=64)
+                t["vis", j] = vwp.tile([P, 2, COLS], U8, tag="vis", name="vis", align_bytes=64)
+            for c0, n in SPLIT:
+                nc.vector.quantize_mx(out=t["viw", j][:, gp, c0:c0 + n].bitcast(FP8X4),
+                                      scales=t["vis", j][:, gp, c0:c0 + n],
+                                      in_=t["gv", j][:, gp, 4 * c0:4 * (c0 + n)])
+
+        def meanp(k):
+            if k == 0:
+                for hf in range(2):
+                    t["ups", hf] = psum.tile([P, 512], F32, tag="ps", name="u_ps")
+            for tt in range(3 * k, min(3 * k + 3, T)):
+                for hf in range(2):
+                    nc.tensor.matmul(out=t["ups", hf][:], lhsT=ident_b[:],
+                                     rhs=t["vq", k][:, tt - 3 * k, 512 * hf:512 * hf + 512],
+                                     start=(tt == 0), stop=(tt == T - 1))
+
+        def uev():
+            for hf in range(2):
+                nc.scalar.mul(out=u_sb[:, 512 * hf:512 * hf + 512], in_=t["ups", hf][:], mul=1.0 / T)
+
+        def ut(gp):
+            bank = psum.tile([P, 4, B], F32, tag="ps", name="ubank")
+            t["ub", gp] = bank
+            u_cols = u_sb[:].rearrange("b (a p e) -> b a e p", p=P, e=2)
+            for k in range(4):
+                m = 4 * gp + k
+                nc.tensor.transpose(bank[:, k, :], u_cols[:, m // 2, m % 2, :], ident_f[:])
+
+        def eu(gp):
+            if gp == 0:
+                t["gu"] = gwp.tile([P, 2, B, 4], BF16, tag="gw", name="gu", align_bytes=64)
+            nc.vector.tensor_copy(out=t["gu"][:, gp], in_=t["ub", gp][:].rearrange("p t b -> p b t"))
+
+        def qu():
+            nc.vector.quantize_mx(out=uw[:].bitcast(FP8X4), scales=us[:],
+                                  in_=t["gu"][:].rearrange("p g b t -> p (g b t)"))
+
+        def m3(h):
+            ps = psum.tile([P, 4, B], F32, tag="ps", name="ps3")
+            t["p3", h] = ps
+            for mi in range(4):
+                m = 4 * h + mi
+                for gp in range(2):
+                    nc.tensor.matmul_mx(
+                        out=ps[:, mi, :],
+                        lhsT=words["wu"][:, gp, P * m:P * m + P].bitcast(FP8X4),
+                        lhsT_scale=planes["wu"][:, gp, P * m:P * m + P],
+                        rhs=uw[:, B * gp:B * gp + B].bitcast(FP8X4),
+                        rhs_scale=us[:, B * gp:B * gp + B],
+                        start=(gp == 0), stop=(gp == 1))
+
+        def vqt_out(h):
+            for mi in range(4):
+                m = 4 * h + mi
+                if mi % 2 == 0:
+                    nc.scalar.activation(out=vqt[:, m, :], in_=t["p3", h][:, mi, :], func=ACT.Identity,
+                                         bias=bu[:, m:m + 1], scale=1.0)
+                else:
+                    nc.vector.tensor_scalar_add(out=vqt[:, m, :], in0=t["p3", h][:, mi, :],
+                                                scalar1=bu[:, m:m + 1])
+
+        def m2(j, m):
+            ps = psum.tile([P, COLS], F32, tag="ps", name="ps2")
+            t["p2", j, m] = ps
+            for c0, n in SPLIT:
+                for gp in range(2):
+                    nc.tensor.matmul_mx(
+                        out=ps[:, c0:c0 + n],
+                        lhsT=words["wv"][:, gp, P * m:P * m + P].bitcast(FP8X4),
+                        lhsT_scale=planes["wv"][:, gp, P * m:P * m + P],
+                        rhs=t["viw", j][:, gp, c0:c0 + n].bitcast(FP8X4),
+                        rhs_scale=t["vis", j][:, gp, c0:c0 + n],
+                        start=(gp == 0), stop=(gp == 1))
+
+        def add(j, m):
+            if m % Q == 0:
+                t["z", j, m // Q] = b6.tile([P, Q, COLS], F32, tag="b6", name="z", align_bytes=64)
+            nc.vector.tensor_tensor(
+                out=t["z", j, m // Q][:, m % Q, :].rearrange("p (b s) -> p b s", s=S),
+                in0=t["p2", j, m][:].rearrange("p (b s) -> p b s", s=S),
+                in1=vqt[:, m, BJ * j:BJ * j + BJ].unsqueeze(2).to_broadcast([P, BJ, S]),
+                op=ALU.add)
+
+        def te(j, h):
+            z = t["z", j, h]
+            nc.scalar.activation(out=z[:], in_=z[:], func=ACT.Tanh)
+            nc.scalar.activation(out=z[:], in_=z[:], func=ACT.Exp)
+
+        def prod(j, h):
+            t["pr", j, h] = b6.tile([P, Q, COLS], F32, tag="b6", name="pr", align_bytes=64)
+            nc.gpsimd.tensor_tensor(out=t["pr", j, h][:], in0=t["z", j, h][:],
+                                    in1=t["vi", j][:, Q * h:Q * h + Q, :], op=ALU.mult)
+
+        def den(j, h):
+            if h == 0:
+                t["den", j] = small.tile([P, 8 * BJ], F32, tag="den", name="den")
+                t["num", j] = small.tile([P, 8 * BJ], F32, tag="num", name="num")
+            nc.vector.tensor_reduce(out=t["den", j][:, Q * BJ * h:Q * BJ * (h + 1)],
+                                    in_=t["z", j, h][:].rearrange("p m (b s) -> p (m b) s", s=S),
+                                    axis=AX.X, op=ALU.add)
+
+        def num(j, h):
+            nc.vector.tensor_reduce(out=t["num", j][:, Q * BJ * h:Q * BJ * (h + 1)],
+                                    in_=t["pr", j, h][:].rearrange("p m (b s) -> p (m b) s", s=S),
+                                    axis=AX.X, op=ALU.add)
+
+        def finj(j):
+            rden = small.tile([P, 8 * BJ], F32, tag="rden", name="rden")
+            nc.vector.reciprocal(out=rden[:], in_=t["den", j][:])
+            nc.vector.tensor_tensor(out=res[:, :, BJ * j:BJ * j + BJ],
+                                    in0=t["num", j][:].rearrange("p (m b) -> p m b", b=BJ),
+                                    in1=rden[:].rearrange("p (m b) -> p m b", b=BJ),
+                                    op=ALU.mult)
+
+        waiting = []
+        step = [0]
+
+        def later(lag, key, call):
+            if lag <= 0:
+                call()
+            else:
+                waiting.append((step[0] + lag, key, call))
+
+        def write_due(due):
+            keep = []
+            for item in waiting:
+                if due(item):
+                    item[2]()
+                else:
+                    keep.append(item)
+            waiting[:] = keep
+
+        def tick():
+            step[0] += 1
+            write_due(lambda item: item[0] <= step[0])
+
+        def flush():
+            waiting.sort(key=lambda item: item[0])
+            write_due(lambda item: True)
+
+        for a in range(4):
+            ld("x", 2 * a)
+            ld("x", 2 * a + 1)
+            ld("l1", a)
+        nc.vector.tensor_copy(out=lb[:], in_=lb_raw[:])
+        nc.vector.tensor_copy(out=bu[:], in_=bu_raw[:])
+        late = [("vq", k) for k in range(7)] + [("wu", 0), ("wu", 1), ("wv", 0), ("wv", 1)]
+        pattern = (("X", 0, "S"), ("X", 2, "V"), ("X", 1, "S"), ("X", 3, "V"), ("X", 4, "S"),
+                   ("L", 0, "V"), ("X", 5, "S"), ("L", 1, "S"), ("L", 2, "S"), ("L", 3, "S"))
+        for a in range(4):
+            for kind, i, eng in pattern:
+                if kind == "X":
+                    tx(a, i)
+                    ex(a, i, eng)
+                    if i == 5:
+                        for k in range(3):
+                            later(LAG_QX, None, lambda a=a, k=k: qx(a, k))
+                else:
+                    tw("l1", a, i)
+                    ew("l1", a, i, eng)
+                    later(LAG_QW, None, lambda a=a, i=i: qw("l1", a, i))
+                tick()
+            n_b6 = 0
+            n_ldw = 0
+            while late:
+                if late[0][0] == "vq":
+                    if n_b6 == 2:
+                        break
+                    n_b6 += 1
+                else:
+                    if n_ldw == 1:
+                        break
+                    n_ldw += 1
+                ld(late[0][0], late[0][1])
+                late.pop(0)
+        while late:
+            ld(late[0][0], late[0][1])
+            late.pop(0)
+        flush()
+
+        for m in range(4):
+            m1(0, m)
+            th1(0, m)
+        cast(0, 0, "V")
+        for m in range(4, 8):
+            m1(0, m)
+            th1(0, m)
+        qv(0, 0)
+        for k in range(7):
+            meanp(k)
+        cast(0, 1, "V")
+        qv(0, 1)
+        uev()
+        wu_banks = [(a, g) for a in range(4) for g in range(2)]
+        for i, (a, g) in enumerate(wu_banks):
+            if i == 2:
+                ut(0)
+                ut(1)
+            tw("wu", a, g)
+            ew("wu", a, g, "S")
+            if i == 3:
+                eu(0)
+                eu(1)
+                qu()
+            if i >= 2:
+                qw("wu", wu_banks[i - 2][0], wu_banks[i - 2][1])
+        qw("wu", 3, 0)
+        qw("wu", 3, 1)
+        for g in range(2):
+            tw("wv", 0, g)
+            ew("wv", 0, g, "SV"[g])
+        m3(0)
+        m3(1)
+        qw("wv", 0, 0)
+        qw("wv", 0, 1)
+        vqt_out(0)
+        vqt_out(1)
+        for a in range(1, 4):
+            for g in range(2):
+                tw("wv", a, g)
+                ew("wv", a, g, "SV"[g])
+            for g in range(2):
+                qw("wv", a, g)
+
+        m1_units = [(j, m) for j in range(1, 4) for m in range(8)]
+
+        def write_m1():
+            j, m = m1_units.pop(0)
+            m1(j, m)
+            th1(j, m)
+            if m % 4 == 3:
+                later(LAG_CAST, ("feeds", j), lambda: cast(j, m // 4, "G"))
+                later(LAG_CAST + LAG_QV, ("feeds", j), lambda: qv(j, m // 4))
+            tick()
+
+        for i in range(PRE):
+            write_m1()
+        for j in range(4):
+            for m in range(8):
+                while m1_units and m1_units[0][0] <= j:
+                    write_m1()
+                if m == 0:
+                    write_due(lambda item: item[1] == ("feeds", j))
+                m2(j, m)
+                add(j, m)
+                if m % Q == Q - 1:
+                    h = m // Q
+                    later(LAG_TE, None, lambda j=j, h=h: te(j, h))
+                    later(LAG_TE + LAG_PROD, None, lambda j=j, h=h: prod(j, h))
+                    later(LAG_TE + LAG_PROD, None, lambda j=j, h=h: den(j, h))
+                    later(LAG_TE + LAG_PROD + LAG_NUM, None, lambda j=j, h=h: num(j, h))
+                    if m == 7:
+                        later(LAG_TE + LAG_PROD + LAG_NUM, None, lambda j=j: finj(j))
+                tick()
+                if m1_units:
+                    write_m1()
+        flush()
+
+        for k in range(2):
+            fin = psum.tile([P, 2, 2, P], F32, tag="ps", name="fin")
+            for a2 in range(2):
+                for e in range(2):
+                    nc.tensor.transpose(fin[:, a2, e, :], res[:, 4 * k + 2 * a2 + e, :], ident_f[:])
+            nc.vector.tensor_tensor(
+                out=osb[:, 512 * k:512 * k + 512].rearrange("b (a p e) -> b a p e", a=2, e=2),
+                in0=fin[:].rearrange("b a e p -> b a p e"),
+                in1=u_sb[:, 512 * k:512 * k + 512].rearrange("b (a p e) -> b a p e", a=2, e=2),
+                op=ALU.add)
+            nc.sync.dma_start(out=out[:, 512 * k:512 * k + 512], in_=osb[:, 512 * k:512 * k + 512])

@@ -36,7 +36,6 @@ Q = 2
 def tile_attentionmechanism_pa_kernel(tc, v_i, v_q, l1_w, l1_b, w_vi0, w_u0, b_u0, out):
     nc = tc.nc
     with ExitStack() as ctx:
-        ctx.enter_context(tc.manual_schedule())
         const = ctx.enter_context(tc.tile_pool(name="const", bufs=1))
         ldw = ctx.enter_context(tc.tile_pool(name="ldw", bufs=4))
         b6 = ctx.enter_context(tc.tile_pool(name="b6", bufs=8))

@@ -31,6 +31,8 @@ LAG_PROD = 4
 LAG_NUM = 1
 PRE = 2
 Q = 2
+FOLD_FROM = 2
+NG = 3
 
 
 def tile_attentionmechanism_pa_kernel(tc, v_i, v_q, l1_w, l1_b, w_vi0, w_u0, b_u0, out):
@@ -41,7 +43,7 @@ def tile_attentionmechanism_pa_kernel(tc, v_i, v_q, l1_w, l1_b, w_vi0, w_u0, b_u
         b6 = ctx.enter_context(tc.tile_pool(name="b6", bufs=8))
         a12 = ctx.enter_context(tc.tile_pool(name="a12", bufs=3))
         gwp = ctx.enter_context(tc.tile_pool(name="gwp", bufs=4))
-        vwp = ctx.enter_context(tc.tile_pool(name="vwp", bufs=3))
+        vwp = ctx.enter_context(tc.tile_pool(name="vwp", bufs=4))
         small = ctx.enter_context(tc.tile_pool(name="small", bufs=2))
         psum = ctx.enter_context(tc.psum_pool(name="psum", bufs=8))
 
@@ -72,7 +74,9 @@ def tile_attentionmechanism_pa_kernel(tc, v_i, v_q, l1_w, l1_b, w_vi0, w_u0, b_u
         u_sb = const.tile([P, HID], F32, name="u_sb")
         vqt = const.tile([P, 8, B], F32, name="vqt")
         res = const.tile([P, 8, B], F32, name="res")
-        osb = const.tile([P, HID], F32, name="osb")
+        acc = const.tile([P, HID], F32, name="acc")
+        osb = acc
+        gu = const.tile([P, 2, B, 4], BF16, name="gu", align_bytes=64)
 
         t = {}
 
@@ -187,18 +191,33 @@ def tile_attentionmechanism_pa_kernel(tc, v_i, v_q, l1_w, l1_b, w_vi0, w_u0, b_u
                                       in_=t["gv", j][:, gp, 4 * c0:4 * (c0 + n)])
 
         def meanp(k):
-            if k == 0:
+            if k == NG:
                 for hf in range(2):
                     t["ups", hf] = psum.tile([P, 512], F32, tag="ps", name="u_ps")
             for tt in range(3 * k, min(3 * k + 3, T)):
                 for hf in range(2):
                     nc.tensor.matmul(out=t["ups", hf][:], lhsT=ident_b[:],
                                      rhs=t["vq", k][:, tt - 3 * k, 512 * hf:512 * hf + 512],
-                                     start=(tt == 0), stop=(tt == T - 1))
+                                     start=(tt == 3 * NG), stop=(tt == T - 1))
+
+        def meang(k):
+            for i in range(3):
+                if k == 0 and i == 0:
+                    continue
+                if k == 0 and i == 1:
+                    nc.gpsimd.tensor_tensor(out=acc[:], in0=t["vq", 0][:, 0, :], in1=t["vq", 0][:, 1, :],
+                                            op=ALU.add)
+                else:
+                    nc.gpsimd.tensor_tensor(out=acc[:], in0=acc[:], in1=t["vq", k][:, i, :], op=ALU.add)
+            if k == NG - 1:
+                nc.gpsimd.tensor_scalar(out=acc[:], in0=acc[:], scalar1=1.0 / T, scalar2=0.0,
+                                        op0=ALU.mult, op1=ALU.add)
 
         def uev():
             for hf in range(2):
-                nc.scalar.mul(out=u_sb[:, 512 * hf:512 * hf + 512], in_=t["ups", hf][:], mul=1.0 / T)
+                nc.vector.scalar_tensor_tensor(out=u_sb[:, 512 * hf:512 * hf + 512], in0=t["ups", hf][:],
+                                               scalar=1.0 / T, in1=acc[:, 512 * hf:512 * hf + 512],
+                                               op0=ALU.mult, op1=ALU.add)
 
         def ut(gp):
             bank = psum.tile([P, 4, B], F32, tag="ps", name="ubank")
@@ -209,13 +228,25 @@ def tile_attentionmechanism_pa_kernel(tc, v_i, v_q, l1_w, l1_b, w_vi0, w_u0, b_u
                 nc.tensor.transpose(bank[:, k, :], u_cols[:, m // 2, m % 2, :], ident_f[:])
 
         def eu(gp):
-            if gp == 0:
-                t["gu"] = gwp.tile([P, 2, B, 4], BF16, tag="gw", name="gu", align_bytes=64)
-            nc.vector.tensor_copy(out=t["gu"][:, gp], in_=t["ub", gp][:].rearrange("p t b -> p b t"))
+            nc.scalar.copy(out=gu[:, gp], in_=t["ub", gp][:].rearrange("p t b -> p b t"))
 
         def qu():
             nc.vector.quantize_mx(out=uw[:].bitcast(FP8X4), scales=us[:],
-                                  in_=t["gu"][:].rearrange("p g b t -> p (g b t)"))
+                                  in_=gu[:].rearrange("p g b t -> p (g b t)"))
+
+        def rep_u(j):
+            gur = b6.tile([P, 2, COLS * 4], BF16, tag="b6", name="gur", align_bytes=64)
+            t["urw", j] = vwp.tile([P, 2, COLS], U32, tag="viw", name="urw", align_bytes=64)
+            t["urs", j] = vwp.tile([P, 2, COLS], U8, tag="vis", name="urs", align_bytes=64)
+            for gp in range(2):
+                nc.vector.tensor_copy(
+                    out=gur[:, gp, :].rearrange("p (b s t) -> p b s t", s=S, t=4),
+                    in_=gu[:, gp, BJ * j:BJ * j + BJ, :].unsqueeze(2).to_broadcast([P, BJ, S, 4]))
+            for gp in range(2):
+                for c0, n in SPLIT:
+                    nc.vector.quantize_mx(out=t["urw", j][:, gp, c0:c0 + n].bitcast(FP8X4),
+                                          scales=t["urs", j][:, gp, c0:c0 + n],
+                                          in_=gur[:, gp, 4 * c0:4 * (c0 + n)])
 
         def m3(h):
             ps = psum.tile([P, 4, B], F32, tag="ps", name="ps3")
@@ -244,19 +275,27 @@ def tile_attentionmechanism_pa_kernel(tc, v_i, v_q, l1_w, l1_b, w_vi0, w_u0, b_u
         def m2(j, m):
             ps = psum.tile([P, COLS], F32, tag="ps", name="ps2")
             t["p2", j, m] = ps
+            pairs = [("wv", "viw", "vis")]
+            if j >= FOLD_FROM:
+                pairs.append(("wu", "urw", "urs"))
             for c0, n in SPLIT:
-                for gp in range(2):
-                    nc.tensor.matmul_mx(
-                        out=ps[:, c0:c0 + n],
-                        lhsT=words["wv"][:, gp, P * m:P * m + P].bitcast(FP8X4),
-                        lhsT_scale=planes["wv"][:, gp, P * m:P * m + P],
-                        rhs=t["viw", j][:, gp, c0:c0 + n].bitcast(FP8X4),
-                        rhs_scale=t["vis", j][:, gp, c0:c0 + n],
-                        start=(gp == 0), stop=(gp == 1))
+                for i, (w, rw, rs) in enumerate(pairs):
+                    for gp in range(2):
+                        nc.tensor.matmul_mx(
+                            out=ps[:, c0:c0 + n],
+                            lhsT=words[w][:, gp, P * m:P * m + P].bitcast(FP8X4),
+                            lhsT_scale=planes[w][:, gp, P * m:P * m + P],
+                            rhs=t[rw, j][:, gp, c0:c0 + n].bitcast(FP8X4),
+                            rhs_scale=t[rs, j][:, gp, c0:c0 + n],
+                            start=(i == 0 and gp == 0), stop=(i == len(pairs) - 1 and gp == 1))
 
         def add(j, m):
             if m % Q == 0:
                 t["z", j, m // Q] = b6.tile([P, Q, COLS], F32, tag="b6", name="z", align_bytes=64)
+            if j >= FOLD_FROM:
+                nc.scalar.activation(out=t["z", j, m // Q][:, m % Q, :], in_=t["p2", j, m][:], func=ACT.Tanh,
+                                     bias=bu[:, m:m + 1], scale=1.0)
+                return
             nc.vector.tensor_tensor(
                 out=t["z", j, m // Q][:, m % Q, :].rearrange("p (b s) -> p b s", s=S),
                 in0=t["p2", j, m][:].rearrange("p (b s) -> p b s", s=S),
@@ -265,7 +304,8 @@ def tile_attentionmechanism_pa_kernel(tc, v_i, v_q, l1_w, l1_b, w_vi0, w_u0, b_u
 
         def te(j, h):
             z = t["z", j, h]
-            nc.scalar.activation(out=z[:], in_=z[:], func=ACT.Tanh)
+            if j < FOLD_FROM:
+                nc.scalar.activation(out=z[:], in_=z[:], func=ACT.Tanh)
             nc.scalar.activation(out=z[:], in_=z[:], func=ACT.Exp)
 
         def prod(j, h):
@@ -320,13 +360,16 @@ def tile_attentionmechanism_pa_kernel(tc, v_i, v_q, l1_w, l1_b, w_vi0, w_u0, b_u
             waiting.sort(key=lambda item: item[0])
             write_due(lambda item: True)
 
-        for a in range(4):
+        for a in range(3):
             ld("x", 2 * a)
             ld("x", 2 * a + 1)
             ld("l1", a)
+            if a > 0:
+                ld("vq", a - 1)
         nc.vector.tensor_copy(out=lb[:], in_=lb_raw[:])
         nc.vector.tensor_copy(out=bu[:], in_=bu_raw[:])
-        late = [("vq", k) for k in range(7)] + [("wu", 0), ("wu", 1), ("wv", 0), ("wv", 1)]
+        late = ([("x", 6), ("x", 7), ("l1", 3)] + [("vq", k) for k in range(2, 7)]
+                + [("wu", 0), ("wu", 1), ("wv", 0), ("wv", 1)])
         pattern = (("X", 0, "S"), ("X", 2, "V"), ("X", 1, "S"), ("X", 3, "V"), ("X", 4, "S"),
                    ("L", 0, "V"), ("X", 5, "S"), ("L", 1, "S"), ("L", 2, "S"), ("L", 3, "S"))
         for a in range(4):
@@ -345,7 +388,7 @@ def tile_attentionmechanism_pa_kernel(tc, v_i, v_q, l1_w, l1_b, w_vi0, w_u0, b_u
             n_b6 = 0
             n_ldw = 0
             while late:
-                if late[0][0] == "vq":
+                if late[0][0] in ("vq", "x"):
                     if n_b6 == 2:
                         break
                     n_b6 += 1
@@ -360,17 +403,19 @@ def tile_attentionmechanism_pa_kernel(tc, v_i, v_q, l1_w, l1_b, w_vi0, w_u0, b_u
             late.pop(0)
         flush()
 
+        for k in range(NG):
+            meang(k)
         for m in range(4):
             m1(0, m)
             th1(0, m)
-        cast(0, 0, "V")
+        cast(0, 0, "G")
         for m in range(4, 8):
             m1(0, m)
             th1(0, m)
         qv(0, 0)
-        for k in range(7):
+        for k in range(NG, 7):
             meanp(k)
-        cast(0, 1, "V")
+        cast(0, 1, "G")
         qv(0, 1)
         uev()
         wu_banks = [(a, g) for a in range(4) for g in range(2)]
@@ -390,7 +435,7 @@ def tile_attentionmechanism_pa_kernel(tc, v_i, v_q, l1_w, l1_b, w_vi0, w_u0, b_u
         qw("wu", 3, 1)
         for g in range(2):
             tw("wv", 0, g)
-            ew("wv", 0, g, "SV"[g])
+            ew("wv", 0, g, "S")
         m3(0)
         m3(1)
         qw("wv", 0, 0)
@@ -400,7 +445,7 @@ def tile_attentionmechanism_pa_kernel(tc, v_i, v_q, l1_w, l1_b, w_vi0, w_u0, b_u
         for a in range(1, 4):
             for g in range(2):
                 tw("wv", a, g)
-                ew("wv", a, g, "SV"[g])
+                ew("wv", a, g, "S")
             for g in range(2):
                 qw("wv", a, g)
 
@@ -423,6 +468,11 @@ def tile_attentionmechanism_pa_kernel(tc, v_i, v_q, l1_w, l1_b, w_vi0, w_u0, b_u
                     write_m1()
                 if m == 0:
                     write_due(lambda item: item[1] == ("feeds", j))
+                    if j == 0 and FOLD_FROM <= 1:
+                        for jf in range(FOLD_FROM, 2):
+                            rep_u(jf)
+                    if j + 1 >= max(FOLD_FROM, 2) and j + 1 < NJ:
+                        rep_u(j + 1)
                 m2(j, m)
                 add(j, m)
                 if m % Q == Q - 1:

@@ -31,8 +31,6 @@ LAG_PROD = 4
 LAG_NUM = 1
 PRE = 2
 Q = 2
-FOLD_FROM = 2
-NG = 3
 
 
 def tile_attentionmechanism_pa_kernel(tc, v_i, v_q, l1_w, l1_b, w_vi0, w_u0, b_u0, out):
@@ -43,7 +41,7 @@ def tile_attentionmechanism_pa_kernel(tc, v_i, v_q, l1_w, l1_b, w_vi0, w_u0, b_u
         b6 = ctx.enter_context(tc.tile_pool(name="b6", bufs=8))
         a12 = ctx.enter_context(tc.tile_pool(name="a12", bufs=3))
         gwp = ctx.enter_context(tc.tile_pool(name="gwp", bufs=4))
-        vwp = ctx.enter_context(tc.tile_pool(name="vwp", bufs=4))
+        vwp = ctx.enter_context(tc.tile_pool(name="vwp", bufs=3))
         small = ctx.enter_context(tc.tile_pool(name="small", bufs=2))
         psum = ctx.enter_context(tc.psum_pool(name="psum", bufs=8))
 
@@ -74,9 +72,7 @@ def tile_attentionmechanism_pa_kernel(tc, v_i, v_q, l1_w, l1_b, w_vi0, w_u0, b_u
         u_sb = const.tile([P, HID], F32, name="u_sb")
         vqt = const.tile([P, 8, B], F32, name="vqt")
         res = const.tile([P, 8, B], F32, name="res")
-        acc = const.tile([P, HID], F32, name="acc")
-        osb = acc
-        gu = const.tile([P, 2, B, 4], BF16, name="gu", align_bytes=64)
+        osb = const.tile([P, HID], F32, name="osb")
 
         t = {}
 
@@ -178,46 +174,33 @@ def tile_attentionmechanism_pa_kernel(tc, v_i, v_q, l1_w, l1_b, w_vi0, w_u0, b_u
             if eng == "V":
                 nc.vector.tensor_copy(out=dst, in_=src)
             else:
-                nc.gpsimd.tensor_scalar(out=dst, in0=src, scalar1=1.0, scalar2=0.0,
-                                        op0=ALU.mult, op1=ALU.add)
+                for c0 in (0, COLS // 2):
+                    nc.gpsimd.tensor_scalar(out=dst[:, c0:c0 + COLS // 2, :], in0=src[:, c0:c0 + COLS // 2, :],
+                                            scalar1=1.0, scalar2=0.0, op0=ALU.mult, op1=ALU.add)
 
         def qv(j, gp):
             if gp == 0:
-                t["viw", j] = vwp.tile([P, 2, COLS], U32, tag="viw", name="viw", align_bytes=64)
-                t["vis", j] = vwp.tile([P, 2, COLS], U8, tag="vis", name="vis", align_bytes=64)
-            for c0, n in SPLIT:
-                nc.vector.quantize_mx(out=t["viw", j][:, gp, c0:c0 + n].bitcast(FP8X4),
-                                      scales=t["vis", j][:, gp, c0:c0 + n],
-                                      in_=t["gv", j][:, gp, 4 * c0:4 * (c0 + n)])
+                return
+            t["viw", j] = vwp.tile([P, 2, COLS], U32, tag="viw", name="viw", align_bytes=64)
+            t["vis", j] = vwp.tile([P, 2, COLS], U8, tag="vis", name="vis", align_bytes=64)
+            for c0, n in ((0, 512), (512, 256)):
+                nc.vector.quantize_mx(out=t["viw", j][:].rearrange("p g c -> p (g c)")[:, c0:c0 + n].bitcast(FP8X4),
+                                      scales=t["vis", j][:].rearrange("p g c -> p (g c)")[:, c0:c0 + n],
+                                      in_=t["gv", j][:].rearrange("p g c -> p (g c)")[:, 4 * c0:4 * (c0 + n)])
 
         def meanp(k):
-            if k == NG:
+            if k == 0:
                 for hf in range(2):
                     t["ups", hf] = psum.tile([P, 512], F32, tag="ps", name="u_ps")
             for tt in range(3 * k, min(3 * k + 3, T)):
                 for hf in range(2):
                     nc.tensor.matmul(out=t["ups", hf][:], lhsT=ident_b[:],
                                      rhs=t["vq", k][:, tt - 3 * k, 512 * hf:512 * hf + 512],
-                                     start=(tt == 3 * NG), stop=(tt == T - 1))
-
-        def meang(k):
-            for i in range(3):
-                if k == 0 and i == 0:
-                    continue
-                if k == 0 and i == 1:
-                    nc.gpsimd.tensor_tensor(out=acc[:], in0=t["vq", 0][:, 0, :], in1=t["vq", 0][:, 1, :],
-                                            op=ALU.add)
-                else:
-                    nc.gpsimd.tensor_tensor(out=acc[:], in0=acc[:], in1=t["vq", k][:, i, :], op=ALU.add)
-            if k == NG - 1:
-                nc.gpsimd.tensor_scalar(out=acc[:], in0=acc[:], scalar1=1.0 / T, scalar2=0.0,
-                                        op0=ALU.mult, op1=ALU.add)
+                                     start=(tt == 0), stop=(tt == T - 1))
 
         def uev():
             for hf in range(2):
-                nc.vector.scalar_tensor_tensor(out=u_sb[:, 512 * hf:512 * hf + 512], in0=t["ups", hf][:],
-                                               scalar=1.0 / T, in1=acc[:, 512 * hf:512 * hf + 512],
-                                               op0=ALU.mult, op1=ALU.add)
+                nc.scalar.mul(out=u_sb[:, 512 * hf:512 * hf + 512], in_=t["ups", hf][:], mul=1.0 / T)
 
         def ut(gp):
             bank = psum.tile([P, 4, B], F32, tag="ps", name="ubank")
@@ -228,25 +211,13 @@ def tile_attentionmechanism_pa_kernel(tc, v_i, v_q, l1_w, l1_b, w_vi0, w_u0, b_u
                 nc.tensor.transpose(bank[:, k, :], u_cols[:, m // 2, m % 2, :], ident_f[:])
 
         def eu(gp):
-            nc.scalar.copy(out=gu[:, gp], in_=t["ub", gp][:].rearrange("p t b -> p b t"))
+            if gp == 0:
+                t["gu"] = gwp.tile([P, 2, B, 4], BF16, tag="gw", name="gu", align_bytes=64)
+            nc.scalar.copy(out=t["gu"][:, gp], in_=t["ub", gp][:].rearrange("p t b -> p b t"))
 
         def qu():
             nc.vector.quantize_mx(out=uw[:].bitcast(FP8X4), scales=us[:],
-                                  in_=gu[:].rearrange("p g b t -> p (g b t)"))
-
-        def rep_u(j):
-            gur = b6.tile([P, 2, COLS * 4], BF16, tag="b6", name="gur", align_bytes=64)
-            t["urw", j] = vwp.tile([P, 2, COLS], U32, tag="viw", name="urw", align_bytes=64)
-            t["urs", j] = vwp.tile([P, 2, COLS], U8, tag="vis", name="urs", align_bytes=64)
-            for gp in range(2):
-                nc.vector.tensor_copy(
-                    out=gur[:, gp, :].rearrange("p (b s t) -> p b s t", s=S, t=4),
-                    in_=gu[:, gp, BJ * j:BJ * j + BJ, :].unsqueeze(2).to_broadcast([P, BJ, S, 4]))
-            for gp in range(2):
-                for c0, n in SPLIT:
-                    nc.vector.quantize_mx(out=t["urw", j][:, gp, c0:c0 + n].bitcast(FP8X4),
-                                          scales=t["urs", j][:, gp, c0:c0 + n],
-                                          in_=gur[:, gp, 4 * c0:4 * (c0 + n)])
+                                  in_=t["gu"][:].rearrange("p g b t -> p (g b t)"))
 
         def m3(h):
             ps = psum.tile([P, 4, B], F32, tag="ps", name="ps3")
@@ -275,27 +246,19 @@ def tile_attentionmechanism_pa_kernel(tc, v_i, v_q, l1_w, l1_b, w_vi0, w_u0, b_u
         def m2(j, m):
             ps = psum.tile([P, COLS], F32, tag="ps", name="ps2")
             t["p2", j, m] = ps
-            pairs = [("wv", "viw", "vis")]
-            if j >= FOLD_FROM:
-                pairs.append(("wu", "urw", "urs"))
             for c0, n in SPLIT:
-                for i, (w, rw, rs) in enumerate(pairs):
-                    for gp in range(2):
-                        nc.tensor.matmul_mx(
-                            out=ps[:, c0:c0 + n],
-                            lhsT=words[w][:, gp, P * m:P * m + P].bitcast(FP8X4),
-                            lhsT_scale=planes[w][:, gp, P * m:P * m + P],
-                            rhs=t[rw, j][:, gp, c0:c0 + n].bitcast(FP8X4),
-                            rhs_scale=t[rs, j][:, gp, c0:c0 + n],
-                            start=(i == 0 and gp == 0), stop=(i == len(pairs) - 1 and gp == 1))
+                for gp in range(2):
+                    nc.tensor.matmul_mx(
+                        out=ps[:, c0:c0 + n],
+                        lhsT=words["wv"][:, gp, P * m:P * m + P].bitcast(FP8X4),
+                        lhsT_scale=planes["wv"][:, gp, P * m:P * m + P],
+                        rhs=t["viw", j][:, gp, c0:c0 + n].bitcast(FP8X4),
+                        rhs_scale=t["vis", j][:, gp, c0:c0 + n],
+                        start=(gp == 0), stop=(gp == 1))
 
         def add(j, m):
             if m % Q == 0:
                 t["z", j, m // Q] = b6.tile([P, Q, COLS], F32, tag="b6", name="z", align_bytes=64)
-            if j >= FOLD_FROM:
-                nc.scalar.activation(out=t["z", j, m // Q][:, m % Q, :], in_=t["p2", j, m][:], func=ACT.Tanh,
-                                     bias=bu[:, m:m + 1], scale=1.0)
-                return
             nc.vector.tensor_tensor(
                 out=t["z", j, m // Q][:, m % Q, :].rearrange("p (b s) -> p b s", s=S),
                 in0=t["p2", j, m][:].rearrange("p (b s) -> p b s", s=S),
@@ -304,14 +267,14 @@ def tile_attentionmechanism_pa_kernel(tc, v_i, v_q, l1_w, l1_b, w_vi0, w_u0, b_u
 
         def te(j, h):
             z = t["z", j, h]
-            if j < FOLD_FROM:
-                nc.scalar.activation(out=z[:], in_=z[:], func=ACT.Tanh)
+            nc.scalar.activation(out=z[:], in_=z[:], func=ACT.Tanh)
             nc.scalar.activation(out=z[:], in_=z[:], func=ACT.Exp)
 
         def prod(j, h):
             t["pr", j, h] = b6.tile([P, Q, COLS], F32, tag="b6", name="pr", align_bytes=64)
-            nc.gpsimd.tensor_tensor(out=t["pr", j, h][:], in0=t["z", j, h][:],
-                                    in1=t["vi", j][:, Q * h:Q * h + Q, :], op=ALU.mult)
+            for i in range(Q):
+                nc.gpsimd.tensor_tensor(out=t["pr", j, h][:, i, :], in0=t["z", j, h][:, i, :],
+                                        in1=t["vi", j][:, Q * h + i, :], op=ALU.mult)
 
         def den(j, h):
             if h == 0:
@@ -360,16 +323,13 @@ def tile_attentionmechanism_pa_kernel(tc, v_i, v_q, l1_w, l1_b, w_vi0, w_u0, b_u
             waiting.sort(key=lambda item: item[0])
             write_due(lambda item: True)
 
-        for a in range(3):
+        for a in range(4):
             ld("x", 2 * a)
             ld("x", 2 * a + 1)
             ld("l1", a)
-            if a > 0:
-                ld("vq", a - 1)
         nc.vector.tensor_copy(out=lb[:], in_=lb_raw[:])
         nc.vector.tensor_copy(out=bu[:], in_=bu_raw[:])
-        late = ([("x", 6), ("x", 7), ("l1", 3)] + [("vq", k) for k in range(2, 7)]
-                + [("wu", 0), ("wu", 1), ("wv", 0), ("wv", 1)])
+        late = [("vq", k) for k in range(7)] + [("wu", 0), ("wu", 1), ("wv", 0), ("wv", 1)]
         pattern = (("X", 0, "S"), ("X", 2, "V"), ("X", 1, "S"), ("X", 3, "V"), ("X", 4, "S"),
                    ("L", 0, "V"), ("X", 5, "S"), ("L", 1, "S"), ("L", 2, "S"), ("L", 3, "S"))
         for a in range(4):
@@ -388,7 +348,7 @@ def tile_attentionmechanism_pa_kernel(tc, v_i, v_q, l1_w, l1_b, w_vi0, w_u0, b_u
             n_b6 = 0
             n_ldw = 0
             while late:
-                if late[0][0] in ("vq", "x"):
+                if late[0][0] == "vq":
                     if n_b6 == 2:
                         break
                     n_b6 += 1
@@ -403,19 +363,17 @@ def tile_attentionmechanism_pa_kernel(tc, v_i, v_q, l1_w, l1_b, w_vi0, w_u0, b_u
             late.pop(0)
         flush()
 
-        for k in range(NG):
-            meang(k)
         for m in range(4):
             m1(0, m)
             th1(0, m)
-        cast(0, 0, "G")
+        cast(0, 0, "V")
         for m in range(4, 8):
             m1(0, m)
             th1(0, m)
         qv(0, 0)
-        for k in range(NG, 7):
+        for k in range(7):
             meanp(k)
-        cast(0, 1, "G")
+        cast(0, 1, "V")
         qv(0, 1)
         uev()
         wu_banks = [(a, g) for a in range(4) for g in range(2)]
@@ -468,11 +426,6 @@ def tile_attentionmechanism_pa_kernel(tc, v_i, v_q, l1_w, l1_b, w_vi0, w_u0, b_u
                     write_m1()
                 if m == 0:
                     write_due(lambda item: item[1] == ("feeds", j))
-                    if j == 0 and FOLD_FROM <= 1:
-                        for jf in range(FOLD_FROM, 2):
-                            rep_u(jf)
-                    if j + 1 >= max(FOLD_FROM, 2) and j + 1 < NJ:
-                        rep_u(j + 1)
                 m2(j, m)
                 add(j, m)
                 if m % Q == Q - 1:

@@ -40,8 +40,9 @@ def tile_attentionmechanism_pa_kernel(tc, v_i, v_q, l1_w, l1_b, w_vi0, w_u0, b_u
         ldw = ctx.enter_context(tc.tile_pool(name="ldw", bufs=4))
         b6 = ctx.enter_context(tc.tile_pool(name="b6", bufs=8))
         a12 = ctx.enter_context(tc.tile_pool(name="a12", bufs=3))
-        gwp = ctx.enter_context(tc.tile_pool(name="gwp", bufs=4))
+        gwp = ctx.enter_context(tc.tile_pool(name="gwp", bufs=3))
         vwp = ctx.enter_context(tc.tile_pool(name="vwp", bufs=3))
+        urp = ctx.enter_context(tc.tile_pool(name="urp", bufs=4))
         small = ctx.enter_context(tc.tile_pool(name="small", bufs=2))
         psum = ctx.enter_context(tc.psum_pool(name="psum", bufs=8))
 
@@ -67,12 +68,9 @@ def tile_attentionmechanism_pa_kernel(tc, v_i, v_q, l1_w, l1_b, w_vi0, w_u0, b_u
                   "wu": const.tile([P, 2, HID], U8, name="wus", align_bytes=64)}
         xw = const.tile([P, 4, B * S], U32, name="xw", align_bytes=64)
         xs = const.tile([P, 4, B * S], U8, name="xs", align_bytes=64)
-        uw = const.tile([P, 2 * B], U32, name="uw", align_bytes=64)
-        us = const.tile([P, 2 * B], U8, name="us", align_bytes=64)
         u_sb = const.tile([P, HID], F32, name="u_sb")
-        vqt = const.tile([P, 8, B], F32, name="vqt")
         res = const.tile([P, 8, B], F32, name="res")
-        osb = const.tile([P, HID], F32, name="osb")
+        gu = const.tile([P, 2, B, 4], BF16, name="gu", align_bytes=64)
 
         t = {}
 
@@ -174,19 +172,16 @@ def tile_attentionmechanism_pa_kernel(tc, v_i, v_q, l1_w, l1_b, w_vi0, w_u0, b_u
             if eng == "V":
                 nc.vector.tensor_copy(out=dst, in_=src)
             else:
-                for c0 in (0, COLS // 2):
-                    nc.gpsimd.tensor_scalar(out=dst[:, c0:c0 + COLS // 2, :], in0=src[:, c0:c0 + COLS // 2, :],
-                                            scalar1=1.0, scalar2=0.0, op0=ALU.mult, op1=ALU.add)
+                nc.scalar.copy(out=dst, in_=src)
 
         def qv(j, gp):
             if gp == 0:
-                return
-            t["viw", j] = vwp.tile([P, 2, COLS], U32, tag="viw", name="viw", align_bytes=64)
-            t["vis", j] = vwp.tile([P, 2, COLS], U8, tag="vis", name="vis", align_bytes=64)
-            for c0, n in ((0, 512), (512, 256)):
-                nc.vector.quantize_mx(out=t["viw", j][:].rearrange("p g c -> p (g c)")[:, c0:c0 + n].bitcast(FP8X4),
-                                      scales=t["vis", j][:].rearrange("p g c -> p (g c)")[:, c0:c0 + n],
-                                      in_=t["gv", j][:].rearrange("p g c -> p (g c)")[:, 4 * c0:4 * (c0 + n)])
+                t["viw", j] = vwp.tile([P, 2, COLS], U32, tag="viw", name="viw", align_bytes=64)
+                t["vis", j] = vwp.tile([P, 2, COLS], U8, tag="vis", name="vis", align_bytes=64)
+            for c0, n in SPLIT:
+                nc.vector.quantize_mx(out=t["viw", j][:, gp, c0:c0 + n].bitcast(FP8X4),
+                                      scales=t["vis", j][:, gp, c0:c0 + n],
+                                      in_=t["gv", j][:, gp, 4 * c0:4 * (c0 + n)])
 
         def meanp(k):
             if k == 0:
@@ -211,70 +206,49 @@ def tile_attentionmechanism_pa_kernel(tc, v_i, v_q, l1_w, l1_b, w_vi0, w_u0, b_u
                 nc.tensor.transpose(bank[:, k, :], u_cols[:, m // 2, m % 2, :], ident_f[:])
 
         def eu(gp):
-            if gp == 0:
-                t["gu"] = gwp.tile([P, 2, B, 4], BF16, tag="gw", name="gu", align_bytes=64)
-            nc.scalar.copy(out=t["gu"][:, gp], in_=t["ub", gp][:].rearrange("p t b -> p b t"))
+            nc.scalar.copy(out=gu[:, gp], in_=t["ub", gp][:].rearrange("p t b -> p b t"))
 
-        def qu():
-            nc.vector.quantize_mx(out=uw[:].bitcast(FP8X4), scales=us[:],
-                                  in_=t["gu"][:].rearrange("p g b t -> p (g b t)"))
-
-        def m3(h):
-            ps = psum.tile([P, 4, B], F32, tag="ps", name="ps3")
-            t["p3", h] = ps
-            for mi in range(4):
-                m = 4 * h + mi
-                for gp in range(2):
-                    nc.tensor.matmul_mx(
-                        out=ps[:, mi, :],
-                        lhsT=words["wu"][:, gp, P * m:P * m + P].bitcast(FP8X4),
-                        lhsT_scale=planes["wu"][:, gp, P * m:P * m + P],
-                        rhs=uw[:, B * gp:B * gp + B].bitcast(FP8X4),
-                        rhs_scale=us[:, B * gp:B * gp + B],
-                        start=(gp == 0), stop=(gp == 1))
-
-        def vqt_out(h):
-            for mi in range(4):
-                m = 4 * h + mi
-                if mi % 2 == 0:
-                    nc.scalar.activation(out=vqt[:, m, :], in_=t["p3", h][:, mi, :], func=ACT.Identity,
-                                         bias=bu[:, m:m + 1], scale=1.0)
-                else:
-                    nc.vector.tensor_scalar_add(out=vqt[:, m, :], in0=t["p3", h][:, mi, :],
-                                                scalar1=bu[:, m:m + 1])
+        def rep_u(j):
+            gur = b6.tile([P, 2, COLS * 4], BF16, tag="b6", name="gur", align_bytes=64)
+            t["urw", j] = urp.tile([P, 2, COLS], U32, tag="urw", name="urw", align_bytes=64)
+            t["urs", j] = urp.tile([P, 2, COLS], U8, tag="urs", name="urs", align_bytes=64)
+            for gp in range(2):
+                nc.vector.tensor_copy(
+                    out=gur[:, gp, :].rearrange("p (b s t) -> p b s t", s=S, t=4),
+                    in_=gu[:, gp, BJ * j:BJ * j + BJ, :].unsqueeze(2).to_broadcast([P, BJ, S, 4]))
+            for c0, n in ((0, 512), (512, 256)):
+                nc.vector.quantize_mx(out=t["urw", j][:].rearrange("p g c -> p (g c)")[:, c0:c0 + n].bitcast(FP8X4),
+                                      scales=t["urs", j][:].rearrange("p g c -> p (g c)")[:, c0:c0 + n],
+                                      in_=gur[:].rearrange("p g c -> p (g c)")[:, 4 * c0:4 * (c0 + n)])
 
         def m2(j, m):
             ps = psum.tile([P, COLS], F32, tag="ps", name="ps2")
             t["p2", j, m] = ps
             for c0, n in SPLIT:
-                for gp in range(2):
-                    nc.tensor.matmul_mx(
-                        out=ps[:, c0:c0 + n],
-                        lhsT=words["wv"][:, gp, P * m:P * m + P].bitcast(FP8X4),
-                        lhsT_scale=planes["wv"][:, gp, P * m:P * m + P],
-                        rhs=t["viw", j][:, gp, c0:c0 + n].bitcast(FP8X4),
-                        rhs_scale=t["vis", j][:, gp, c0:c0 + n],
-                        start=(gp == 0), stop=(gp == 1))
+                for i, (w, rw, rs) in enumerate((("wu", "urw", "urs"), ("wv", "viw", "vis"))):
+                    for gp in range(2):
+                        nc.tensor.matmul_mx(
+                            out=ps[:, c0:c0 + n],
+                            lhsT=words[w][:, gp, P * m:P * m + P].bitcast(FP8X4),
+                            lhsT_scale=planes[w][:, gp, P * m:P * m + P],
+                            rhs=t[rw, j][:, gp, c0:c0 + n].bitcast(FP8X4),
+                            rhs_scale=t[rs, j][:, gp, c0:c0 + n],
+                            start=(i == 0 and gp == 0), stop=(i == 1 and gp == 1))
 
         def add(j, m):
             if m % Q == 0:
                 t["z", j, m // Q] = b6.tile([P, Q, COLS], F32, tag="b6", name="z", align_bytes=64)
-            nc.vector.tensor_tensor(
-                out=t["z", j, m // Q][:, m % Q, :].rearrange("p (b s) -> p b s", s=S),
-                in0=t["p2", j, m][:].rearrange("p (b s) -> p b s", s=S),
-                in1=vqt[:, m, BJ * j:BJ * j + BJ].unsqueeze(2).to_broadcast([P, BJ, S]),
-                op=ALU.add)
+            nc.scalar.activation(out=t["z", j, m // Q][:, m % Q, :], in_=t["p2", j, m][:], func=ACT.Tanh,
+                                 bias=bu[:, m:m + 1], scale=1.0)
 
         def te(j, h):
             z = t["z", j, h]
-            nc.scalar.activation(out=z[:], in_=z[:], func=ACT.Tanh)
             nc.scalar.activation(out=z[:], in_=z[:], func=ACT.Exp)
 
         def prod(j, h):
             t["pr", j, h] = b6.tile([P, Q, COLS], F32, tag="b6", name="pr", align_bytes=64)
-            for i in range(Q):
-                nc.gpsimd.tensor_tensor(out=t["pr", j, h][:, i, :], in0=t["z", j, h][:, i, :],
-                                        in1=t["vi", j][:, Q * h + i, :], op=ALU.mult)
+            nc.vector.tensor_tensor(out=t["pr", j, h][:], in0=t["z", j, h][:],
+                                    in1=t["vi", j][:, Q * h:Q * h + Q, :], op=ALU.mult)
 
         def den(j, h):
             if h == 0:
@@ -366,14 +340,14 @@ def tile_attentionmechanism_pa_kernel(tc, v_i, v_q, l1_w, l1_b, w_vi0, w_u0, b_u
         for m in range(4):
             m1(0, m)
             th1(0, m)
-        cast(0, 0, "V")
+        cast(0, 0, "S")
         for m in range(4, 8):
             m1(0, m)
             th1(0, m)
         qv(0, 0)
         for k in range(7):
             meanp(k)
-        cast(0, 1, "V")
+        cast(0, 1, "S")
         qv(0, 1)
         uev()
         wu_banks = [(a, g) for a in range(4) for g in range(2)]
@@ -386,7 +360,7 @@ def tile_attentionmechanism_pa_kernel(tc, v_i, v_q, l1_w, l1_b, w_vi0, w_u0, b_u
             if i == 3:
                 eu(0)
                 eu(1)
-                qu()
+                rep_u(0)
             if i >= 2:
                 qw("wu", wu_banks[i - 2][0], wu_banks[i - 2][1])
         qw("wu", 3, 0)
@@ -394,18 +368,17 @@ def tile_attentionmechanism_pa_kernel(tc, v_i, v_q, l1_w, l1_b, w_vi0, w_u0, b_u
         for g in range(2):
             tw("wv", 0, g)
             ew("wv", 0, g, "S")
-        m3(0)
-        m3(1)
         qw("wv", 0, 0)
         qw("wv", 0, 1)
-        vqt_out(0)
-        vqt_out(1)
         for a in range(1, 4):
             for g in range(2):
                 tw("wv", a, g)
                 ew("wv", a, g, "S")
             for g in range(2):
                 qw("wv", a, g)
+
+        for jf in range(1, NJ):
+            rep_u(jf)
 
         m1_units = [(j, m) for j in range(1, 4) for m in range(8)]
 
@@ -414,7 +387,7 @@ def tile_attentionmechanism_pa_kernel(tc, v_i, v_q, l1_w, l1_b, w_vi0, w_u0, b_u
             m1(j, m)
             th1(j, m)
             if m % 4 == 3:
-                later(LAG_CAST, ("feeds", j), lambda: cast(j, m // 4, "G"))
+                later(LAG_CAST, ("feeds", j), lambda: cast(j, m // 4, "S"))
                 later(LAG_CAST + LAG_QV, ("feeds", j), lambda: qv(j, m // 4))
             tick()
 
@@ -447,8 +420,8 @@ def tile_attentionmechanism_pa_kernel(tc, v_i, v_q, l1_w, l1_b, w_vi0, w_u0, b_u
                 for e in range(2):
                     nc.tensor.transpose(fin[:, a2, e, :], res[:, 4 * k + 2 * a2 + e, :], ident_f[:])
             nc.vector.tensor_tensor(
-                out=osb[:, 512 * k:512 * k + 512].rearrange("b (a p e) -> b a p e", a=2, e=2),
+                out=u_sb[:, 512 * k:512 * k + 512].rearrange("b (a p e) -> b a p e", a=2, e=2),
                 in0=fin[:].rearrange("b a e p -> b a p e"),
                 in1=u_sb[:, 512 * k:512 * k + 512].rearrange("b (a p e) -> b a p e", a=2, e=2),
                 op=ALU.add)
-            nc.sync.dma_start(out=out[:, 512 * k:512 * k + 512], in_=osb[:, 512 * k:512 * k + 512])
+            nc.sync.dma_start(out=out[:, 512 * k:512 * k + 512], in_=u_sb[:, 512 * k:512 * k + 512])

@@ -247,8 +247,9 @@ def tile_attentionmechanism_pa_kernel(tc, v_i, v_q, l1_w, l1_b, w_vi0, w_u0, b_u
 
         def prod(j, h):
             t["pr", j, h] = b6.tile([P, Q, COLS], F32, tag="b6", name="pr", align_bytes=64)
-            nc.vector.tensor_tensor(out=t["pr", j, h][:], in0=t["z", j, h][:],
-                                    in1=t["vi", j][:, Q * h:Q * h + Q, :], op=ALU.mult)
+            eng = nc.gpsimd if j >= 2 else nc.vector
+            eng.tensor_tensor(out=t["pr", j, h][:], in0=t["z", j, h][:],
+                              in1=t["vi", j][:, Q * h:Q * h + Q, :], op=ALU.mult)
 
         def den(j, h):
             if h == 0:
@@ -263,13 +264,26 @@ def tile_attentionmechanism_pa_kernel(tc, v_i, v_q, l1_w, l1_b, w_vi0, w_u0, b_u
                                     in_=t["pr", j, h][:].rearrange("p m (b s) -> p (m b) s", s=S),
                                     axis=AX.X, op=ALU.add)
 
-        def finj(j):
+        def finj(j, m0, m1):
             rden = small.tile([P, 8 * BJ], F32, tag="rden", name="rden")
-            nc.vector.reciprocal(out=rden[:], in_=t["den", j][:])
-            nc.vector.tensor_tensor(out=res[:, :, BJ * j:BJ * j + BJ],
-                                    in0=t["num", j][:].rearrange("p (m b) -> p m b", b=BJ),
-                                    in1=rden[:].rearrange("p (m b) -> p m b", b=BJ),
+            cols = slice(BJ * m0, BJ * m1)
+            nc.vector.reciprocal(out=rden[:, cols], in_=t["den", j][:, cols])
+            nc.vector.tensor_tensor(out=res[:, m0:m1, BJ * j:BJ * j + BJ],
+                                    in0=t["num", j][:, cols].rearrange("p (m b) -> p m b", b=BJ),
+                                    in1=rden[:, cols].rearrange("p (m b) -> p m b", b=BJ),
                                     op=ALU.mult)
+
+        def final(k):
+            fin = psum.tile([P, 2, 2, P], F32, tag="ps", name="fin")
+            for a2 in range(2):
+                for e in range(2):
+                    nc.tensor.transpose(fin[:, a2, e, :], res[:, 4 * k + 2 * a2 + e, :], ident_f[:])
+            nc.vector.tensor_tensor(
+                out=u_sb[:, 512 * k:512 * k + 512].rearrange("b (a p e) -> b a p e", a=2, e=2),
+                in0=fin[:].rearrange("b a e p -> b a p e"),
+                in1=u_sb[:, 512 * k:512 * k + 512].rearrange("b (a p e) -> b a p e", a=2, e=2),
+                op=ALU.add)
+            nc.sync.dma_start(out=out[:, 512 * k:512 * k + 512], in_=u_sb[:, 512 * k:512 * k + 512])
 
         waiting = []
         step = [0]
@@ -407,21 +421,12 @@ def tile_attentionmechanism_pa_kernel(tc, v_i, v_q, l1_w, l1_b, w_vi0, w_u0, b_u
                     later(LAG_TE + LAG_PROD, None, lambda j=j, h=h: prod(j, h))
                     later(LAG_TE + LAG_PROD, None, lambda j=j, h=h: den(j, h))
                     later(LAG_TE + LAG_PROD + LAG_NUM, None, lambda j=j, h=h: num(j, h))
-                    if m == 7:
-                        later(LAG_TE + LAG_PROD + LAG_NUM, None, lambda j=j: finj(j))
+                    if m == 7 and j < NJ - 1:
+                        later(LAG_TE + LAG_PROD + LAG_NUM, None, lambda j=j: finj(j, 0, 8))
+                    if m % 4 == 3 and j == NJ - 1:
+                        later(LAG_TE + LAG_PROD + LAG_NUM, None, lambda j=j, m=m: finj(j, m - 3, m + 1))
+                        later(LAG_TE + LAG_PROD + LAG_NUM, None, lambda m=m: final(m // 4))
                 tick()
                 if m1_units:
                     write_m1()
         flush()
-
-        for k in range(2):
-            fin = psum.tile([P, 2, 2, P], F32, tag="ps", name="fin")
-            for a2 in range(2):
-                for e in range(2):
-                    nc.tensor.transpose(fin[:, a2, e, :], res[:, 4 * k + 2 * a2 + e, :], ident_f[:])
-            nc.vector.tensor_tensor(
-                out=u_sb[:, 512 * k:512 * k + 512].rearrange("b (a p e) -> b a p e", a=2, e=2),
-                in0=fin[:].rearrange("b a e p -> b a p e"),
-                in1=u_sb[:, 512 * k:512 * k + 512].rearrange("b (a p e) -> b a p e", a=2, e=2),
-                op=ALU.add)
-            nc.sync.dma_start(out=out[:, 512 * k:512 * k + 512], in_=u_sb[:, 512 * k:512 * k + 512])

@@ -31,6 +31,7 @@ LAG_PROD = 4
 LAG_NUM = 1
 PRE = 2
 Q = 2
+NV = 2
 
 
 def tile_attentionmechanism_pa_kernel(tc, v_i, v_q, l1_w, l1_b, w_vi0, w_u0, b_u0, out):
@@ -184,18 +185,30 @@ def tile_attentionmechanism_pa_kernel(tc, v_i, v_q, l1_w, l1_b, w_vi0, w_u0, b_u
                                       in_=t["gv", j][:, gp, 4 * c0:4 * (c0 + n)])
 
         def meanp(k):
-            if k == 0:
+            if k == NV:
                 for hf in range(2):
                     t["ups", hf] = psum.tile([P, 512], F32, tag="ps", name="u_ps")
             for tt in range(3 * k, min(3 * k + 3, T)):
                 for hf in range(2):
                     nc.tensor.matmul(out=t["ups", hf][:], lhsT=ident_b[:],
                                      rhs=t["vq", k][:, tt - 3 * k, 512 * hf:512 * hf + 512],
-                                     start=(tt == 0), stop=(tt == T - 1))
+                                     start=(tt == 3 * NV), stop=(tt == T - 1))
+
+        def meanv(k):
+            if k == 0:
+                t["acc"] = b6.tile([P, HID], F32, tag="b6", name="acc", align_bytes=64)
+                nc.vector.tensor_tensor(out=t["acc"][:], in0=t["vq", 0][:, 0, :], in1=t["vq", 0][:, 1, :],
+                                        op=ALU.add)
+            for i in range(2 if k == 0 else 0, 3):
+                nc.vector.tensor_tensor(out=t["acc"][:], in0=t["acc"][:], in1=t["vq", k][:, i, :], op=ALU.add)
+            if k == NV - 1:
+                nc.vector.tensor_scalar_mul(out=t["acc"][:], in0=t["acc"][:], scalar1=1.0 / T)
 
         def uev():
             for hf in range(2):
-                nc.scalar.mul(out=u_sb[:, 512 * hf:512 * hf + 512], in_=t["ups", hf][:], mul=1.0 / T)
+                nc.vector.scalar_tensor_tensor(out=u_sb[:, 512 * hf:512 * hf + 512], in0=t["ups", hf][:],
+                                               scalar=1.0 / T, in1=t["acc"][:, 512 * hf:512 * hf + 512],
+                                               op0=ALU.mult, op1=ALU.add)
 
         def ut(gp):
             bank = psum.tile([P, 4, B], F32, tag="ps", name="ubank")
@@ -351,6 +364,8 @@ def tile_attentionmechanism_pa_kernel(tc, v_i, v_q, l1_w, l1_b, w_vi0, w_u0, b_u
             late.pop(0)
         flush()
 
+        for k in range(NV):
+            meanv(k)
         for m in range(4):
             m1(0, m)
             th1(0, m)
@@ -359,7 +374,7 @@ def tile_attentionmechanism_pa_kernel(tc, v_i, v_q, l1_w, l1_b, w_vi0, w_u0, b_u
             m1(0, m)
             th1(0, m)
         qv(0, 0)
-        for k in range(7):
+        for k in range(NV, 7):
             meanp(k)
         cast(0, 1, "S")
         qv(0, 1)

@@ -16,34 +16,26 @@ P = 128
 B, C, S, T, HID = 128, 2048, 12, 20, 1024
 FLOPS = 2 * B * S * HID * C + 2 * B * S * HID * HID + 2 * B * HID * HID
 
-NJ = 4
-BJ = B // NJ
-COLS = BJ * S
-SPLIT = ((0, 256), (256, 128))
-
-
-LAG_QW = 2
-LAG_QX = 1
-LAG_CAST = 1
-LAG_QV = 3
-LAG_TE = 2
-LAG_PROD = 4
-LAG_NUM = 1
-PRE = 2
-Q = 2
-NV = 2
+NI, NJ = 3, 4
+COLS = B * NJ
+EARLY = 0
+VSET = (0, 1, 2, 3)
+LAG_Q, LAG_CAST, LAG_QV, LAG_EXP, LAG_DEN, LAG_NUM, LAG_FIN = 2, 2, 2, 2, 1, 3, 6
+CAST_ON = "VVVVVV"
+X_ON = "SVSVSS"
+L1_ON = "VSSS"
+W_ON = "SS"
 
 
 def tile_attentionmechanism_pa_kernel(tc, v_i, v_q, l1_w, l1_b, w_vi0, w_u0, b_u0, out):
     nc = tc.nc
     with ExitStack() as ctx:
         const = ctx.enter_context(tc.tile_pool(name="const", bufs=1))
-        ldw = ctx.enter_context(tc.tile_pool(name="ldw", bufs=4))
-        b6 = ctx.enter_context(tc.tile_pool(name="b6", bufs=8))
-        a12 = ctx.enter_context(tc.tile_pool(name="a12", bufs=3))
-        gwp = ctx.enter_context(tc.tile_pool(name="gwp", bufs=3))
-        vwp = ctx.enter_context(tc.tile_pool(name="vwp", bufs=3))
-        urp = ctx.enter_context(tc.tile_pool(name="urp", bufs=4))
+        k8 = ctx.enter_context(tc.tile_pool(name="k8", bufs=8))
+        b6 = ctx.enter_context(tc.tile_pool(name="b6", bufs=6))
+        k12 = ctx.enter_context(tc.tile_pool(name="k12", bufs=2))
+        gwp = ctx.enter_context(tc.tile_pool(name="gwp", bufs=2))
+        big = ctx.enter_context(tc.tile_pool(name="big", bufs=1))
         small = ctx.enter_context(tc.tile_pool(name="small", bufs=2))
         psum = ctx.enter_context(tc.psum_pool(name="psum", bufs=8))
 
@@ -67,8 +59,12 @@ def tile_attentionmechanism_pa_kernel(tc, v_i, v_q, l1_w, l1_b, w_vi0, w_u0, b_u
         planes = {"l1": const.tile([P, 4, HID], U8, name="l1s", align_bytes=64),
                   "wv": const.tile([P, 2, HID], U8, name="wvs", align_bytes=64),
                   "wu": const.tile([P, 2, HID], U8, name="wus", align_bytes=64)}
-        xw = const.tile([P, 4, B * S], U32, name="xw", align_bytes=64)
-        xs = const.tile([P, 4, B * S], U8, name="xs", align_bytes=64)
+        xw = big.tile([P, 4, NI * COLS], U32, tag="big", name="xw", align_bytes=64)
+        xs = const.tile([P, 4, NI * COLS], U8, name="xs", align_bytes=64)
+        viw = const.tile([P, 2, NI * COLS], U32, name="viw", align_bytes=64)
+        vis = const.tile([P, 2, NI * COLS], U8, name="vis", align_bytes=64)
+        urw = const.tile([P, 2, COLS], U32, name="urw", align_bytes=64)
+        urs = const.tile([P, 2, COLS], U8, name="urs", align_bytes=64)
         u_sb = const.tile([P, HID], F32, name="u_sb")
         res = const.tile([P, 8, B], F32, name="res")
         gu = const.tile([P, 2, B, 4], BF16, name="gu", align_bytes=64)
@@ -77,12 +73,12 @@ def tile_attentionmechanism_pa_kernel(tc, v_i, v_q, l1_w, l1_b, w_vi0, w_u0, b_u
 
         l1_rows = l1_w.rearrange("(a p e) c -> a p e c", p=P, e=2)
         x_flat = v_i.rearrange("b c h w -> b (c h w)")
-        w_rows = {"wu": w_u0.rearrange("(k a p e) c -> k p a e c", a=2, p=P, e=2),
-                  "wv": w_vi0.rearrange("(k a p e) c -> k p a e c", a=2, p=P, e=2)}
+        w_rows = {"wu": w_u0.rearrange("(a p e) c -> a p e c", p=P, e=2),
+                  "wv": w_vi0.rearrange("(a p e) c -> a p e c", p=P, e=2)}
 
         def ld(what, i):
             if what == "l1":
-                t["l1", i] = ldw.tile([P, 2, C], BF16, tag="ldw", name="l1sb")
+                t["l1", i] = k8.tile([P, 2, C], BF16, tag="k8", name="l1sb", align_bytes=64)
                 nc.sync.dma_start(out=t["l1", i][:], in_=l1_rows[i])
             elif what == "x":
                 t["x", i] = b6.tile([P, 256 * S], BF16, tag="b6", name="xq", align_bytes=64)
@@ -92,13 +88,11 @@ def tile_attentionmechanism_pa_kernel(tc, v_i, v_q, l1_w, l1_b, w_vi0, w_u0, b_u
                 t["vq", i] = b6.tile([P, 3, HID], BF16, tag="b6", name="vq", align_bytes=64)
                 nc.sync.dma_start(out=t["vq", i][:, 0:nt, :], in_=v_q[:, 3 * i:3 * i + nt, :])
             else:
-                t[what, i] = ldw.tile([P, 2, 2, HID], BF16, tag="ldw", name="wsb")
+                t[what, i] = b6.tile([P, 2, HID], BF16, tag="b6", name="wsb", align_bytes=64)
                 nc.sync.dma_start(out=t[what, i][:], in_=w_rows[what][i])
 
         def rows_of(w, a, e):
-            if w == "l1":
-                return t["l1", a][:, e, :]
-            return t[w, a // 2][:, a % 2, e, :]
+            return t[w, a][:, e, :]
 
         def copy_on(eng, dst, src):
             if eng == "V":
@@ -117,7 +111,7 @@ def tile_attentionmechanism_pa_kernel(tc, v_i, v_q, l1_w, l1_b, w_vi0, w_u0, b_u
                         ident_f[:])
 
         def ew(w, a, g, eng):
-            gw = gwp.tile([P, 1024], BF16, tag="gw", name="gw", align_bytes=64)
+            gw = gwp.tile([P, 1024], BF16, tag="gw" + eng, bufs=2 if eng == "V" else 3, name="gw", align_bytes=64)
             t["gw", w, a, g] = gw
             copy_on(eng, gw[:].bitcast(F32).rearrange("p (c u) -> p c u", u=2),
                     t["wb", w, a, g][:].rearrange("p u e h -> p (e h) u"))
@@ -127,88 +121,81 @@ def tile_attentionmechanism_pa_kernel(tc, v_i, v_q, l1_w, l1_b, w_vi0, w_u0, b_u
                                   scales=planes[w][:, g, 256 * a:256 * a + 256],
                                   in_=t["gw", w, a, g][:])
 
-        def tx(g, i):
+        def tx(g, k):
             bank = psum.tile([P, 4, P], F32, tag="ps", name="xbank")
-            t["xb", g, i] = bank
+            t["xb", g, k] = bank
             for u in range(2):
-                xv = t["x", 2 * g + u][:].bitcast(F32).rearrange("b (p e i) -> b e i p", p=P, e=2, i=6)
+                xv = t["x", 2 * g + u][:].bitcast(F32).rearrange("b (p e k) -> b e k p", p=P, e=2, k=6)
                 for e in range(2):
-                    nc.tensor.transpose(bank[:, 2 * u + e, :], xv[:, e, i, :], ident_f[:])
+                    nc.tensor.transpose(bank[:, 2 * u + e, :], xv[:, e, k, :], ident_f[:])
 
-        def ex(g, i, eng):
-            if ("gx", g) not in t:
-                t["gx", g] = a12.tile([P, B * S * 4], BF16, tag="a12", name="gx", align_bytes=64)
-            gxv = t["gx", g][:].rearrange("p (b i r t) -> p i b r t", b=B, i=6, r=2, t=4)
-            copy_on(eng, gxv[:, i], t["xb", g, i][:].bitcast(BF16).rearrange("p t (b r) -> p b r t", r=2))
+        def ex(g, k, eng):
+            if k == 0:
+                t["gx", g] = k12.tile([P, NI * COLS * 4], BF16, tag="k12", name="gx", align_bytes=64)
+            gxv = t["gx", g][:].rearrange("p (i b k r t) -> p i k b r t", i=NI, b=B, k=2, r=2, t=4)
+            copy_on(eng, gxv[:, k // 2, k % 2], t["xb", g, k][:].bitcast(BF16).rearrange("p t (b r) -> p b r t", r=2))
 
-        def qx(g, k):
-            nc.vector.quantize_mx(out=xw[:, g, 512 * k:512 * k + 512].bitcast(FP8X4),
-                                  scales=xs[:, g, 512 * k:512 * k + 512],
-                                  in_=t["gx", g][:, 2048 * k:2048 * k + 2048])
+        def qx(g, i):
+            nc.vector.quantize_mx(out=xw[:, g, COLS * i:COLS * i + COLS].bitcast(FP8X4),
+                                  scales=xs[:, g, COLS * i:COLS * i + COLS],
+                                  in_=t["gx", g][:, 4 * COLS * i:4 * COLS * (i + 1)])
 
-        def m1(j, m):
-            ps = psum.tile([P, COLS], F32, tag="ps", name="ps1")
-            t["p1", j, m] = ps
-            for c0, n in SPLIT:
-                for g in range(4):
-                    nc.tensor.matmul_mx(
-                        out=ps[:, c0:c0 + n],
-                        lhsT=words["l1"][:, g, P * m:P * m + P].bitcast(FP8X4),
-                        lhsT_scale=planes["l1"][:, g, P * m:P * m + P],
-                        rhs=xw[:, g, COLS * j + c0:COLS * j + c0 + n].bitcast(FP8X4),
-                        rhs_scale=xs[:, g, COLS * j + c0:COLS * j + c0 + n],
-                        start=(g == 0), stop=(g == 3))
+        def m1(i, m, g):
+            if g == 0:
+                t["p1", i, m] = psum.tile([P, COLS], F32, tag="ps", name="ps1")
+            nc.tensor.matmul_mx(
+                out=t["p1", i, m][:],
+                lhsT=words["l1"][:, g, P * m:P * m + P].bitcast(FP8X4),
+                lhsT_scale=planes["l1"][:, g, P * m:P * m + P],
+                rhs=xw[:, g, COLS * i:COLS * i + COLS].bitcast(FP8X4),
+                rhs_scale=xs[:, g, COLS * i:COLS * i + COLS],
+                start=(g == 0), stop=(g == 3))
 
-        def th1(j, m):
-            if m == 0:
-                t["vi", j] = a12.tile([P, 8, COLS], F32, tag="a12", name="vi", align_bytes=64)
-            nc.scalar.activation(out=t["vi", j][:, m, :], in_=t["p1", j, m][:], func=ACT.Tanh,
+        def th1(i, m):
+            if m % 4 == 0:
+                t["vi", i, m // 4] = k8.tile([P, 4, COLS], F32, tag="k8", name="vi", align_bytes=64)
+            nc.scalar.activation(out=t["vi", i, m // 4][:, m % 4, :], in_=t["p1", i, m][:], func=ACT.Tanh,
                                  bias=lb[:, m:m + 1], scale=1.0)
 
-        def cast(j, gp, eng):
-            if gp == 0:
-                t["gv", j] = b6.tile([P, 2, COLS * 4], BF16, tag="b6", name="gv", align_bytes=64)
-            dst = t["gv", j][:, gp, :].rearrange("p (c t) -> p c t", t=4)
-            src = t["vi", j][:, 4 * gp:4 * gp + 4, :].rearrange("p t c -> p c t")
-            if eng == "V":
-                nc.vector.tensor_copy(out=dst, in_=src)
-            else:
-                nc.scalar.copy(out=dst, in_=src)
+        def cast(i, gp, eng):
+            if i == 0:
+                t["gv", gp] = k12.tile([P, NI, COLS * 4], BF16, tag="k12", name="gv", align_bytes=64)
+            copy_on(eng, t["gv", gp][:, i, :].rearrange("p (c t) -> p c t", t=4),
+                    t["vi", i, gp][:].rearrange("p t c -> p c t"))
 
-        def qv(j, gp):
-            if gp == 0:
-                t["viw", j] = vwp.tile([P, 2, COLS], U32, tag="viw", name="viw", align_bytes=64)
-                t["vis", j] = vwp.tile([P, 2, COLS], U8, tag="vis", name="vis", align_bytes=64)
-            for c0, n in SPLIT:
-                nc.vector.quantize_mx(out=t["viw", j][:, gp, c0:c0 + n].bitcast(FP8X4),
-                                      scales=t["vis", j][:, gp, c0:c0 + n],
-                                      in_=t["gv", j][:, gp, 4 * c0:4 * (c0 + n)])
+        def qv(i, gp):
+            nc.vector.quantize_mx(out=viw[:, gp, COLS * i:COLS * i + COLS].bitcast(FP8X4),
+                                  scales=vis[:, gp, COLS * i:COLS * i + COLS],
+                                  in_=t["gv", gp][:, i, :])
+
+        pe_steps = [tt for tt in range(T) if tt // 3 not in VSET]
 
         def meanp(k):
-            if k == NV:
-                for hf in range(2):
-                    t["ups", hf] = psum.tile([P, 512], F32, tag="ps", name="u_ps")
             for tt in range(3 * k, min(3 * k + 3, T)):
                 for hf in range(2):
+                    if tt == pe_steps[0]:
+                        t["ups", hf] = psum.tile([P, 512], F32, tag="ps", name="u_ps")
                     nc.tensor.matmul(out=t["ups", hf][:], lhsT=ident_b[:],
                                      rhs=t["vq", k][:, tt - 3 * k, 512 * hf:512 * hf + 512],
-                                     start=(tt == 3 * NV), stop=(tt == T - 1))
+                                     start=(tt == pe_steps[0]), stop=(tt == pe_steps[-1]))
+
+        def add_step(k, i):
+            first = t["vq", k][:, 0, :] if (k, i) == (VSET[0], 1) else u_sb[:]
+            nc.vector.tensor_tensor(out=u_sb[:], in0=first, in1=t["vq", k][:, i, :], op=ALU.add)
 
         def meanv(k):
-            if k == 0:
-                t["acc"] = b6.tile([P, HID], F32, tag="b6", name="acc", align_bytes=64)
-                nc.vector.tensor_tensor(out=t["acc"][:], in0=t["vq", 0][:, 0, :], in1=t["vq", 0][:, 1, :],
-                                        op=ALU.add)
-            for i in range(2 if k == 0 else 0, 3):
-                nc.vector.tensor_tensor(out=t["acc"][:], in0=t["acc"][:], in1=t["vq", k][:, i, :], op=ALU.add)
-            if k == NV - 1:
-                nc.vector.tensor_scalar_mul(out=t["acc"][:], in0=t["acc"][:], scalar1=1.0 / T)
+            for i in range(1 if k == VSET[0] else 0, min(3, T - 3 * k)):
+                fill.append(lambda i=i: add_step(k, i))
+            if k == VSET[-1]:
+                fill.append(lambda: nc.vector.tensor_scalar_mul(out=u_sb[:], in0=u_sb[:], scalar1=1.0 / T))
 
         def uev():
+            while fill:
+                fill_one()
             for hf in range(2):
-                nc.vector.scalar_tensor_tensor(out=u_sb[:, 512 * hf:512 * hf + 512], in0=t["ups", hf][:],
-                                               scalar=1.0 / T, in1=t["acc"][:, 512 * hf:512 * hf + 512],
-                                               op0=ALU.mult, op1=ALU.add)
+                cols = slice(512 * hf, 512 * hf + 512)
+                nc.vector.scalar_tensor_tensor(out=u_sb[:, cols], in0=t["ups", hf][:], scalar=1.0 / T,
+                                               in1=u_sb[:, cols], op0=ALU.mult, op1=ALU.add)
 
         def ut(gp):
             bank = psum.tile([P, 4, B], F32, tag="ps", name="ubank")
@@ -221,227 +208,192 @@ def tile_attentionmechanism_pa_kernel(tc, v_i, v_q, l1_w, l1_b, w_vi0, w_u0, b_u
         def eu(gp):
             nc.scalar.copy(out=gu[:, gp], in_=t["ub", gp][:].rearrange("p t b -> p b t"))
 
-        def rep_u(j):
-            gur = b6.tile([P, 2, COLS * 4], BF16, tag="b6", name="gur", align_bytes=64)
-            t["urw", j] = urp.tile([P, 2, COLS], U32, tag="urw", name="urw", align_bytes=64)
-            t["urs", j] = urp.tile([P, 2, COLS], U8, tag="urs", name="urs", align_bytes=64)
-            for gp in range(2):
-                nc.vector.tensor_copy(
-                    out=gur[:, gp, :].rearrange("p (b s t) -> p b s t", s=S, t=4),
-                    in_=gu[:, gp, BJ * j:BJ * j + BJ, :].unsqueeze(2).to_broadcast([P, BJ, S, 4]))
-            for c0, n in ((0, 512), (512, 256)):
-                nc.vector.quantize_mx(out=t["urw", j][:].rearrange("p g c -> p (g c)")[:, c0:c0 + n].bitcast(FP8X4),
-                                      scales=t["urs", j][:].rearrange("p g c -> p (g c)")[:, c0:c0 + n],
-                                      in_=gur[:].rearrange("p g c -> p (g c)")[:, 4 * c0:4 * (c0 + n)])
+        def rep_u(gp):
+            if gp == 0:
+                t["gur"] = k8.tile([P, 2, B, NJ, 4], BF16, tag="k8", name="gur", align_bytes=64)
+            nc.vector.tensor_copy(out=t["gur"][:, gp], in_=gu[:, gp].unsqueeze(2).to_broadcast([P, B, NJ, 4]))
 
-        def m2(j, m):
+        def qu(gp):
+            nc.vector.quantize_mx(out=urw[:, gp, :].bitcast(FP8X4), scales=urs[:, gp, :],
+                                  in_=t["gur"][:, gp].rearrange("p b j t -> p (b j t)"))
+
+        def m2(i, m):
             ps = psum.tile([P, COLS], F32, tag="ps", name="ps2")
-            t["p2", j, m] = ps
-            for c0, n in SPLIT:
-                for i, (w, rw, rs) in enumerate((("wu", "urw", "urs"), ("wv", "viw", "vis"))):
-                    for gp in range(2):
-                        nc.tensor.matmul_mx(
-                            out=ps[:, c0:c0 + n],
-                            lhsT=words[w][:, gp, P * m:P * m + P].bitcast(FP8X4),
-                            lhsT_scale=planes[w][:, gp, P * m:P * m + P],
-                            rhs=t[rw, j][:, gp, c0:c0 + n].bitcast(FP8X4),
-                            rhs_scale=t[rs, j][:, gp, c0:c0 + n],
-                            start=(i == 0 and gp == 0), stop=(i == 1 and gp == 1))
+            t["p2", i, m] = ps
+            cols = slice(COLS * i, COLS * i + COLS)
+            for k in range(4):
+                gp = k % 2
+                w = "wu" if k < 2 else "wv"
+                nc.tensor.matmul_mx(
+                    out=ps[:],
+                    lhsT=words[w][:, gp, P * m:P * m + P].bitcast(FP8X4),
+                    lhsT_scale=planes[w][:, gp, P * m:P * m + P],
+                    rhs=(urw[:, gp, :] if k < 2 else viw[:, gp, cols]).bitcast(FP8X4),
+                    rhs_scale=urs[:, gp, :] if k < 2 else vis[:, gp, cols],
+                    start=(k == 0), stop=(k == 3))
 
-        def add(j, m):
-            if m % Q == 0:
-                t["z", j, m // Q] = b6.tile([P, Q, COLS], F32, tag="b6", name="z", align_bytes=64)
-            nc.scalar.activation(out=t["z", j, m // Q][:, m % Q, :], in_=t["p2", j, m][:], func=ACT.Tanh,
+        def th2(i, m):
+            if i == 0 and m == 0:
+                t["zs"] = big.tile([P, 4, NI, COLS], F32, tag="big", name="zs", align_bytes=64)
+            if i == 0:
+                t["z", m] = t["zs"][:, m % 4]
+            nc.scalar.activation(out=t["z", m][:, i, :], in_=t["p2", i, m][:], func=ACT.Tanh,
                                  bias=bu[:, m:m + 1], scale=1.0)
 
-        def te(j, h):
-            z = t["z", j, h]
-            nc.scalar.activation(out=z[:], in_=z[:], func=ACT.Exp)
+        def te(m, i0, i1):
+            nc.scalar.activation(out=t["z", m][:, i0:i1, :], in_=t["z", m][:, i0:i1, :], func=ACT.Exp)
 
-        def prod(j, h):
-            t["pr", j, h] = b6.tile([P, Q, COLS], F32, tag="b6", name="pr", align_bytes=64)
-            eng = nc.gpsimd if j >= 2 else nc.vector
-            eng.tensor_tensor(out=t["pr", j, h][:], in0=t["z", j, h][:],
-                              in1=t["vi", j][:, Q * h:Q * h + Q, :], op=ALU.mult)
+        def prod(i, m, eng):
+            if i == 0:
+                t["pr", m] = b6.tile([P, NI, COLS], F32, tag="b6", name="pr", align_bytes=64)
+            on = nc.gpsimd if eng == "G" else nc.vector
+            on.tensor_tensor(out=t["pr", m][:, i, :], in0=t["z", m][:, i, :],
+                             in1=t["vi", i, m // 4][:, m % 4, :], op=ALU.mult)
 
-        def den(j, h):
-            if h == 0:
-                t["den", j] = small.tile([P, 8 * BJ], F32, tag="den", name="den")
-                t["num", j] = small.tile([P, 8 * BJ], F32, tag="num", name="num")
-            nc.vector.tensor_reduce(out=t["den", j][:, Q * BJ * h:Q * BJ * (h + 1)],
-                                    in_=t["z", j, h][:].rearrange("p m (b s) -> p (m b) s", s=S),
-                                    axis=AX.X, op=ALU.add)
+        def over_s(dst, src):
+            nc.vector.tensor_reduce(out=dst, in_=src.rearrange("p i (b j) -> p b i j", j=NJ), axis=AX.XY, op=ALU.add)
 
-        def num(j, h):
-            nc.vector.tensor_reduce(out=t["num", j][:, Q * BJ * h:Q * BJ * (h + 1)],
-                                    in_=t["pr", j, h][:].rearrange("p m (b s) -> p (m b) s", s=S),
-                                    axis=AX.X, op=ALU.add)
+        def den(m):
+            t["den", m] = small.tile([P, B], F32, tag="den", name="den")
+            over_s(t["den", m][:], t["z", m])
 
-        def finj(j, m0, m1):
-            rden = small.tile([P, 8 * BJ], F32, tag="rden", name="rden")
-            cols = slice(BJ * m0, BJ * m1)
-            nc.vector.reciprocal(out=rden[:, cols], in_=t["den", j][:, cols])
-            nc.vector.tensor_tensor(out=res[:, m0:m1, BJ * j:BJ * j + BJ],
-                                    in0=t["num", j][:, cols].rearrange("p (m b) -> p m b", b=BJ),
-                                    in1=rden[:, cols].rearrange("p (m b) -> p m b", b=BJ),
-                                    op=ALU.mult)
+        def num(m):
+            t["num", m] = small.tile([P, B], F32, tag="num", name="num")
+            over_s(t["num", m][:], t["pr", m][:])
+            t["rden", m] = small.tile([P, B], F32, tag="rden", name="rden")
+            nc.vector.reciprocal(out=t["rden", m][:], in_=t["den", m][:])
+
+        def quot(m):
+            nc.vector.tensor_tensor(out=res[:, m, :], in0=t["num", m][:], in1=t["rden", m][:], op=ALU.mult)
 
         def final(k):
-            fin = psum.tile([P, 2, 2, P], F32, tag="ps", name="fin")
-            for a2 in range(2):
-                for e in range(2):
-                    nc.tensor.transpose(fin[:, a2, e, :], res[:, 4 * k + 2 * a2 + e, :], ident_f[:])
-            nc.vector.tensor_tensor(
-                out=u_sb[:, 512 * k:512 * k + 512].rearrange("b (a p e) -> b a p e", a=2, e=2),
-                in0=fin[:].rearrange("b a e p -> b a p e"),
-                in1=u_sb[:, 512 * k:512 * k + 512].rearrange("b (a p e) -> b a p e", a=2, e=2),
-                op=ALU.add)
-            nc.sync.dma_start(out=out[:, 512 * k:512 * k + 512], in_=u_sb[:, 512 * k:512 * k + 512])
+            fin = psum.tile([P, 2, P], F32, tag="ps", name="fin")
+            for e in range(2):
+                nc.tensor.transpose(fin[:, e, :], res[:, 2 * k + e, :], ident_f[:])
+            cols = u_sb[:, 256 * k:256 * k + 256]
+            nc.vector.tensor_tensor(out=cols.rearrange("b (p e) -> b p e", e=2),
+                                    in0=fin[:].rearrange("b e p -> b p e"),
+                                    in1=cols.rearrange("b (p e) -> b p e", e=2), op=ALU.add)
+            nc.sync.dma_start(out=out[:, 256 * k:256 * k + 256], in_=cols)
+
 
         waiting = []
         step = [0]
 
-        def later(lag, key, call):
-            if lag <= 0:
-                call()
-            else:
-                waiting.append((step[0] + lag, key, call))
+        def later(lag, call):
+            waiting.append((step[0] + lag, call))
 
-        def write_due(due):
-            keep = []
-            for item in waiting:
-                if due(item):
-                    item[2]()
-                else:
-                    keep.append(item)
-            waiting[:] = keep
+        def write_due(limit):
+            due = [item for item in waiting if item[0] <= limit]
+            waiting[:] = [item for item in waiting if item[0] > limit]
+            for item in due:
+                item[1]()
 
         def tick():
             step[0] += 1
-            write_due(lambda item: item[0] <= step[0])
+            write_due(step[0])
 
-        def flush():
-            waiting.sort(key=lambda item: item[0])
-            write_due(lambda item: True)
+        fill = []
 
-        for a in range(4):
-            ld("x", 2 * a)
-            ld("x", 2 * a + 1)
-            ld("l1", a)
+        def fill_one():
+            if fill:
+                fill.pop(0)()
+
+        ctx.enter_context(tc.manual_schedule())
+        for what, k in (("x", 0), ("x", 1), ("l1", 0), ("x", 2), ("x", 3), ("l1", 1), ("x", 4), ("x", 5), ("x", 6), ("x", 7), ("l1", 2), ("l1", 3)):
+            ld(what, k)
+        for k in range(7):
+            ld("vq", k)
+        for w in ("wu", "wv"):
+            for k in range(4):
+                ld(w, k)
         nc.vector.tensor_copy(out=lb[:], in_=lb_raw[:])
         nc.vector.tensor_copy(out=bu[:], in_=bu_raw[:])
-        late = [("vq", k) for k in range(7)] + [("wu", 0), ("wu", 1), ("wv", 0), ("wv", 1)]
-        pattern = (("X", 0, "S"), ("X", 2, "V"), ("X", 1, "S"), ("X", 3, "V"), ("X", 4, "S"),
-                   ("L", 0, "V"), ("X", 5, "S"), ("L", 1, "S"), ("L", 2, "S"), ("L", 3, "S"))
-        for a in range(4):
-            for kind, i, eng in pattern:
-                if kind == "X":
-                    tx(a, i)
-                    ex(a, i, eng)
-                    if i == 5:
-                        for k in range(3):
-                            later(LAG_QX, None, lambda a=a, k=k: qx(a, k))
-                else:
-                    tw("l1", a, i)
-                    ew("l1", a, i, eng)
-                    later(LAG_QW, None, lambda a=a, i=i: qw("l1", a, i))
-                tick()
-            n_b6 = 0
-            n_ldw = 0
-            while late:
-                if late[0][0] == "vq":
-                    if n_b6 == 2:
-                        break
-                    n_b6 += 1
-                else:
-                    if n_ldw == 1:
-                        break
-                    n_ldw += 1
-                ld(late[0][0], late[0][1])
-                late.pop(0)
-        while late:
-            ld(late[0][0], late[0][1])
-            late.pop(0)
-        flush()
+        early = [(n % NI, n // NI) for n in range(EARLY)]
 
-        for k in range(NV):
-            meanv(k)
-        for m in range(4):
-            m1(0, m)
-            th1(0, m)
-        cast(0, 0, "S")
-        for m in range(4, 8):
-            m1(0, m)
-            th1(0, m)
-        qv(0, 0)
-        for k in range(NV, 7):
-            meanp(k)
-        cast(0, 1, "S")
-        qv(0, 1)
-        uev()
-        wu_banks = [(a, g) for a in range(4) for g in range(2)]
-        for i, (a, g) in enumerate(wu_banks):
-            if i == 2:
-                ut(0)
-                ut(1)
-            tw("wu", a, g)
-            ew("wu", a, g, "S")
-            if i == 3:
-                eu(0)
-                eu(1)
-                rep_u(0)
-            if i >= 2:
-                qw("wu", wu_banks[i - 2][0], wu_banks[i - 2][1])
-        qw("wu", 3, 0)
-        qw("wu", 3, 1)
-        for g in range(2):
-            tw("wv", 0, g)
-            ew("wv", 0, g, "S")
-        qw("wv", 0, 0)
-        qw("wv", 0, 1)
-        for a in range(1, 4):
-            for g in range(2):
-                tw("wv", a, g)
-                ew("wv", a, g, "S")
-            for g in range(2):
-                qw("wv", a, g)
-
-        for jf in range(1, NJ):
-            rep_u(jf)
-
-        m1_units = [(j, m) for j in range(1, 4) for m in range(8)]
-
-        def write_m1():
-            j, m = m1_units.pop(0)
-            m1(j, m)
-            th1(j, m)
-            if m % 4 == 3:
-                later(LAG_CAST, ("feeds", j), lambda: cast(j, m // 4, "S"))
-                later(LAG_CAST + LAG_QV, ("feeds", j), lambda: qv(j, m // 4))
+        def x_bank(g, k):
+            tx(g, k)
+            ex(g, k, X_ON[k])
+            if k % 2 == 1:
+                later(LAG_Q, lambda: qx(g, k // 2))
             tick()
 
-        for i in range(PRE):
-            write_m1()
-        for j in range(4):
-            for m in range(8):
-                while m1_units and m1_units[0][0] <= j:
-                    write_m1()
-                if m == 0:
-                    write_due(lambda item: item[1] == ("feeds", j))
-                m2(j, m)
-                add(j, m)
-                if m % Q == Q - 1:
-                    h = m // Q
-                    later(LAG_TE, None, lambda j=j, h=h: te(j, h))
-                    later(LAG_TE + LAG_PROD, None, lambda j=j, h=h: prod(j, h))
-                    later(LAG_TE + LAG_PROD, None, lambda j=j, h=h: den(j, h))
-                    later(LAG_TE + LAG_PROD + LAG_NUM, None, lambda j=j, h=h: num(j, h))
-                    if m == 7 and j < NJ - 1:
-                        later(LAG_TE + LAG_PROD + LAG_NUM, None, lambda j=j: finj(j, 0, 8))
-                    if m % 4 == 3 and j == NJ - 1:
-                        later(LAG_TE + LAG_PROD + LAG_NUM, None, lambda j=j, m=m: finj(j, m - 3, m + 1))
-                        later(LAG_TE + LAG_PROD + LAG_NUM, None, lambda m=m: final(m // 4))
-                tick()
-                if m1_units:
-                    write_m1()
-        flush()
+        def w_bank(w, a, g, on):
+            tw(w, a, g)
+            ew(w, a, g, on)
+            later(LAG_Q, lambda: qw(w, a, g))
+            tick()
+
+        def unit1(i, m):
+            for g in range(3 if (i, m) in early else 0, 4):
+                m1(i, m, g)
+            th1(i, m)
+            if m % 4 == 3:
+                gp = m // 4
+                later(LAG_CAST, lambda: cast(i, gp, CAST_ON[3 * gp + i]))
+                later(LAG_CAST + LAG_QV, lambda: qv(i, gp))
+            fill_one()
+            tick()
+
+        def unit2(i, m):
+            m2(i, m)
+            th2(i, m)
+            later(LAG_EXP, lambda: te(m, i, i + 1))
+            later(LAG_EXP, lambda: prod(i, m, "G"))
+            if i == 2:
+                later(LAG_EXP + LAG_DEN, lambda: den(m))
+                later(LAG_EXP + LAG_NUM, lambda: num(m))
+                later(LAG_EXP + LAG_NUM + 1, lambda: quot(m))
+                if m % 2 == 1:
+                    later(LAG_EXP + LAG_NUM + LAG_FIN, lambda: final(m // 2))
+            tick()
+
+        def passes(g):
+            for i, m in early:
+                m1(i, m, g)
+
+        x_order = (0, 1, 2, 3)
+        for g in range(4):
+            for k in range(6):
+                x_bank(g, k)
+            if g >= 1:
+                passes(g - 1)
+            if g != 2:
+                a = min(g, 2)
+                for k in range(4):
+                    w_bank("l1", a, k, L1_ON[k])
+
+        for k in VSET:
+            meanv(k)
+        for m in range(4):
+            for i in range(NI):
+                unit1(i, m)
+            if m == 0:
+                for g in range(4):
+                    w_bank("l1", 3, g, L1_ON[g])
+            if m == 2:
+                for k in range(7):
+                    if k not in VSET:
+                        meanp(k)
+                uev()
+        w_after = ((), (("wu", 0),), (), (("wu", 1),), (("wu", 2),), (("wu", 3),), (("wv", 0),), (("wv", 1),), (("wv", 2),), (("wv", 3),), (), ())
+        for n in range(12):
+            if n == 4:
+                for gp in range(2):
+                    ut(gp)
+                    eu(gp)
+            if n == 6:
+                for gp in range(2):
+                    rep_u(gp)
+                    qu(gp)
+            unit1(n // 4, 4 + n % 4)
+            for w, a in w_after[n]:
+                for g in range(2):
+                    w_bank(w, a, g, W_ON[g])
+
+        write_due(step[0] + LAG_CAST + LAG_QV)
+        for m in range(8):
+            for i in range(NI):
+                unit2(i, m)
+        while waiting:
+            tick()

@@ -18,9 +18,13 @@ FLOPS = 2 * B * S * HID * C + 2 * B * S * HID * HID + 2 * B * HID * HID
 
 NI, NJ = 3, 4
 COLS = B * NJ
-EARLY = 0
-VSET = (0, 1, 2, 3)
-LAG_Q, LAG_CAST, LAG_QV, LAG_EXP, LAG_DEN, LAG_NUM, LAG_FIN = 2, 2, 2, 2, 1, 3, 6
+EARLY = 3
+VSET = (0, 1, 2)
+HEAD = (("l1", 0), ("x", 0), ("x", 1), ("l1", 1), ("x", 2), ("x", 3), ("l1", 2))
+FILL_AT = 3
+HALF, L3_AT, MEAN_AT, UEV_AT, UT_AT, REP_AT = 1, 5, 8, 8, 16, 17
+W_AT = (15, 15, 15, 15, 17, 19, 21, 23)
+LAG_Q, LAG_CAST, LAG_QV, LAG_EXP, LAG_DEN, LAG_NUM, LAG_FIN = 3, 1, 2, 2, 1, 4, 4
 CAST_ON = "VVVVVV"
 X_ON = "SVSVSS"
 L1_ON = "VSSS"
@@ -31,8 +35,8 @@ def tile_attentionmechanism_pa_kernel(tc, v_i, v_q, l1_w, l1_b, w_vi0, w_u0, b_u
     nc = tc.nc
     with ExitStack() as ctx:
         const = ctx.enter_context(tc.tile_pool(name="const", bufs=1))
-        k8 = ctx.enter_context(tc.tile_pool(name="k8", bufs=8))
-        b6 = ctx.enter_context(tc.tile_pool(name="b6", bufs=6))
+        k8 = ctx.enter_context(tc.tile_pool(name="k8", bufs=6))
+        b6 = ctx.enter_context(tc.tile_pool(name="b6", bufs=8))
         k12 = ctx.enter_context(tc.tile_pool(name="k12", bufs=2))
         gwp = ctx.enter_context(tc.tile_pool(name="gwp", bufs=2))
         big = ctx.enter_context(tc.tile_pool(name="big", bufs=1))
@@ -79,7 +83,9 @@ def tile_attentionmechanism_pa_kernel(tc, v_i, v_q, l1_w, l1_b, w_vi0, w_u0, b_u
         def ld(what, i):
             if what == "l1":
                 t["l1", i] = k8.tile([P, 2, C], BF16, tag="k8", name="l1sb", align_bytes=64)
-                nc.sync.dma_start(out=t["l1", i][:], in_=l1_rows[i])
+                n = C // 4 if i == 0 else C
+                for c0 in range(0, C, n):
+                    nc.sync.dma_start(out=t["l1", i][:, :, c0:c0 + n], in_=l1_rows[i][:, :, c0:c0 + n])
             elif what == "x":
                 t["x", i] = b6.tile([P, 256 * S], BF16, tag="b6", name="xq", align_bytes=64)
                 nc.sync.dma_start(out=t["x", i][:], in_=x_flat[:, 256 * S * i:256 * S * (i + 1)])
@@ -157,11 +163,12 @@ def tile_attentionmechanism_pa_kernel(tc, v_i, v_q, l1_w, l1_b, w_vi0, w_u0, b_u
             nc.scalar.activation(out=t["vi", i, m // 4][:, m % 4, :], in_=t["p1", i, m][:], func=ACT.Tanh,
                                  bias=lb[:, m:m + 1], scale=1.0)
 
-        def cast(i, gp, eng):
-            if i == 0:
+        def cast(i, gp, h, eng):
+            if i == 0 and h == 0:
                 t["gv", gp] = k12.tile([P, NI, COLS * 4], BF16, tag="k12", name="gv", align_bytes=64)
-            copy_on(eng, t["gv", gp][:, i, :].rearrange("p (c t) -> p c t", t=4),
-                    t["vi", i, gp][:].rearrange("p t c -> p c t"))
+            n = COLS // 2
+            copy_on(eng, t["gv", gp][:, i, 4 * n * h:4 * n * (h + 1)].rearrange("p (c t) -> p c t", t=4),
+                    t["vi", i, gp][:, :, n * h:n * h + n].rearrange("p t c -> p c t"))
 
         def qv(i, gp):
             nc.vector.quantize_mx(out=viw[:, gp, COLS * i:COLS * i + COLS].bitcast(FP8X4),
@@ -192,6 +199,8 @@ def tile_attentionmechanism_pa_kernel(tc, v_i, v_q, l1_w, l1_b, w_vi0, w_u0, b_u
         def uev():
             while fill:
                 fill_one()
+            if not pe_steps:
+                return
             for hf in range(2):
                 cols = slice(512 * hf, 512 * hf + 512)
                 nc.vector.scalar_tensor_tensor(out=u_sb[:, cols], in0=t["ups", hf][:], scalar=1.0 / T,
@@ -209,13 +218,12 @@ def tile_attentionmechanism_pa_kernel(tc, v_i, v_q, l1_w, l1_b, w_vi0, w_u0, b_u
             nc.scalar.copy(out=gu[:, gp], in_=t["ub", gp][:].rearrange("p t b -> p b t"))
 
         def rep_u(gp):
-            if gp == 0:
-                t["gur"] = k8.tile([P, 2, B, NJ, 4], BF16, tag="k8", name="gur", align_bytes=64)
-            nc.vector.tensor_copy(out=t["gur"][:, gp], in_=gu[:, gp].unsqueeze(2).to_broadcast([P, B, NJ, 4]))
+            t["gur", gp] = b6.tile([P, B, NJ, 4], BF16, tag="b6", name="gur", align_bytes=64)
+            nc.vector.tensor_copy(out=t["gur", gp][:], in_=gu[:, gp].unsqueeze(2).to_broadcast([P, B, NJ, 4]))
 
         def qu(gp):
             nc.vector.quantize_mx(out=urw[:, gp, :].bitcast(FP8X4), scales=urs[:, gp, :],
-                                  in_=t["gur"][:, gp].rearrange("p b j t -> p (b j t)"))
+                                  in_=t["gur", gp][:].rearrange("p b j t -> p (b j t)"))
 
         def m2(i, m):
             ps = psum.tile([P, COLS], F32, tag="ps", name="ps2")
@@ -254,17 +262,22 @@ def tile_attentionmechanism_pa_kernel(tc, v_i, v_q, l1_w, l1_b, w_vi0, w_u0, b_u
             nc.vector.tensor_reduce(out=dst, in_=src.rearrange("p i (b j) -> p b i j", j=NJ), axis=AX.XY, op=ALU.add)
 
         def den(m):
-            t["den", m] = small.tile([P, B], F32, tag="den", name="den")
-            over_s(t["den", m][:], t["z", m])
+            if m % 2 == 0:
+                t["den", m // 2] = small.tile([P, 2, B], F32, tag="den", name="den")
+            over_s(t["den", m // 2][:, m % 2, :], t["z", m])
 
         def num(m):
-            t["num", m] = small.tile([P, B], F32, tag="num", name="num")
-            over_s(t["num", m][:], t["pr", m][:])
-            t["rden", m] = small.tile([P, B], F32, tag="rden", name="rden")
-            nc.vector.reciprocal(out=t["rden", m][:], in_=t["den", m][:])
+            if m % 2 == 0:
+                t["num", m // 2] = small.tile([P, 2, B], F32, tag="num", name="num")
+            else:
+                d = t["den", m // 2]
+                nc.vector.reciprocal(out=d[:], in_=d[:])
+            over_s(t["num", m // 2][:, m % 2, :], t["pr", m][:])
 
         def quot(m):
-            nc.vector.tensor_tensor(out=res[:, m, :], in0=t["num", m][:], in1=t["rden", m][:], op=ALU.mult)
+            if m % 2 == 1:
+                nc.vector.tensor_tensor(out=res[:, m - 1:m + 1, :], in0=t["num", m // 2][:], in1=t["den", m // 2][:],
+                                        op=ALU.mult)
 
         def final(k):
             fin = psum.tile([P, 2, P], F32, tag="ps", name="fin")
@@ -283,15 +296,12 @@ def tile_attentionmechanism_pa_kernel(tc, v_i, v_q, l1_w, l1_b, w_vi0, w_u0, b_u
         def later(lag, call):
             waiting.append((step[0] + lag, call))
 
-        def write_due(limit):
-            due = [item for item in waiting if item[0] <= limit]
-            waiting[:] = [item for item in waiting if item[0] > limit]
-            for item in due:
-                item[1]()
-
         def tick():
             step[0] += 1
-            write_due(step[0])
+            due = [item for item in waiting if item[0] <= step[0]]
+            waiting[:] = [item for item in waiting if item[0] > step[0]]
+            for item in due:
+                item[1]()
 
         fill = []
 
@@ -300,16 +310,20 @@ def tile_attentionmechanism_pa_kernel(tc, v_i, v_q, l1_w, l1_b, w_vi0, w_u0, b_u
                 fill.pop(0)()
 
         ctx.enter_context(tc.manual_schedule())
-        for what, k in (("x", 0), ("x", 1), ("l1", 0), ("x", 2), ("x", 3), ("l1", 1), ("x", 4), ("x", 5), ("x", 6), ("x", 7), ("l1", 2), ("l1", 3)):
-            ld(what, k)
+        for what, k in HEAD + (("l1", 3),):
+            if what == "x":
+                ld("x", 2 * k)
+                ld("x", 2 * k + 1)
+            else:
+                ld("l1", k)
         for k in range(7):
             ld("vq", k)
-        for w in ("wu", "wv"):
-            for k in range(4):
-                ld(w, k)
+        for k in range(4):
+            ld("wu", k)
+        for k in range(4):
+            ld("wv", k)
         nc.vector.tensor_copy(out=lb[:], in_=lb_raw[:])
         nc.vector.tensor_copy(out=bu[:], in_=bu_raw[:])
-        early = [(n % NI, n // NI) for n in range(EARLY)]
 
         def x_bank(g, k):
             tx(g, k)
@@ -324,14 +338,18 @@ def tile_attentionmechanism_pa_kernel(tc, v_i, v_q, l1_w, l1_b, w_vi0, w_u0, b_u
             later(LAG_Q, lambda: qw(w, a, g))
             tick()
 
+        units = [(i, m) for m in range(4) for i in range(NI)] + [(i, m) for i in range(NI) for m in range(4, 8)]
+        early = units[:EARLY]
+
         def unit1(i, m):
             for g in range(3 if (i, m) in early else 0, 4):
                 m1(i, m, g)
             th1(i, m)
             if m % 4 == 3:
                 gp = m // 4
-                later(LAG_CAST, lambda: cast(i, gp, CAST_ON[3 * gp + i]))
-                later(LAG_CAST + LAG_QV, lambda: qv(i, gp))
+                for h in range(2):
+                    later(LAG_CAST + h * HALF, lambda h=h: cast(i, gp, h, CAST_ON[3 * gp + i]))
+                later(LAG_CAST + HALF + LAG_QV, lambda: qv(i, gp))
             fill_one()
             tick()
 
@@ -348,50 +366,45 @@ def tile_attentionmechanism_pa_kernel(tc, v_i, v_q, l1_w, l1_b, w_vi0, w_u0, b_u
                     later(LAG_EXP + LAG_NUM + LAG_FIN, lambda: final(m // 2))
             tick()
 
-        def passes(g):
-            for i, m in early:
-                m1(i, m, g)
-
-        x_order = (0, 1, 2, 3)
-        for g in range(4):
+        for what, g in HEAD:
+            if what == "l1":
+                for k in range(4):
+                    w_bank("l1", g, k, L1_ON[k])
+                continue
             for k in range(6):
                 x_bank(g, k)
             if g >= 1:
-                passes(g - 1)
-            if g != 2:
-                a = min(g, 2)
-                for k in range(4):
-                    w_bank("l1", a, k, L1_ON[k])
-
-        for k in VSET:
-            meanv(k)
-        for m in range(4):
-            for i in range(NI):
-                unit1(i, m)
-            if m == 0:
+                for i, m in early:
+                    m1(i, m, g - 1)
+        w_groups = [(w, a) for w in ("wu", "wv") for a in range(4)]
+        for n, (i, m) in enumerate(units):
+            unit1(i, m)
+            if n == FILL_AT:
+                for k in VSET:
+                    meanv(k)
+            if n == L3_AT:
                 for g in range(4):
                     w_bank("l1", 3, g, L1_ON[g])
-            if m == 2:
+            if n == MEAN_AT:
                 for k in range(7):
                     if k not in VSET:
                         meanp(k)
+            if n == UEV_AT:
                 uev()
-        w_after = ((), (("wu", 0),), (), (("wu", 1),), (("wu", 2),), (("wu", 3),), (("wv", 0),), (("wv", 1),), (("wv", 2),), (("wv", 3),), (), ())
-        for n in range(12):
-            if n == 4:
+            if n == UT_AT:
                 for gp in range(2):
                     ut(gp)
                     eu(gp)
-            if n == 6:
+            if n == REP_AT:
                 for gp in range(2):
                     rep_u(gp)
                     qu(gp)
-            unit1(n // 4, 4 + n % 4)
-            for w, a in w_after[n]:
+            for k in range(W_AT.count(n)):
+                w, a = w_groups.pop(0)
                 for g in range(2):
                     w_bank(w, a, g, W_ON[g])
-
-        write_due(step[0] + LAG_CAST + LAG_QV)
+        while [item for item in waiting]:
+            tick()
         for m in range(8):
             for i in range(NI):
                 unit2(i, m)

@@ -242,24 +242,24 @@ def tile_attentionmechanism_pa_kernel(tc, v_i, v_q, l1_w, l1_b, w_vi0, w_u0, b_u
 
         def th2(i, m):
             if i == 0 and m == 0:
-                t["zs"] = big.tile([P, 4, NI, COLS], F32, tag="big", name="zs", align_bytes=64)
+                t["zs"] = big.tile([P, 4, B, NI, NJ], F32, tag="big", name="zs", align_bytes=64)
             if i == 0:
                 t["z", m] = t["zs"][:, m % 4]
-            nc.scalar.activation(out=t["z", m][:, i, :], in_=t["p2", i, m][:], func=ACT.Tanh,
-                                 bias=bu[:, m:m + 1], scale=1.0)
+            nc.scalar.activation(out=t["z", m][:, :, i, :], in_=t["p2", i, m][:].rearrange("p (b j) -> p b j", j=NJ),
+                                 func=ACT.Tanh, bias=bu[:, m:m + 1], scale=1.0)
 
         def te(m, i0, i1):
-            nc.scalar.activation(out=t["z", m][:, i0:i1, :], in_=t["z", m][:, i0:i1, :], func=ACT.Exp)
+            nc.scalar.activation(out=t["z", m][:, :, i0:i1, :], in_=t["z", m][:, :, i0:i1, :], func=ACT.Exp)
 
         def prod(i, m, eng):
             if i == 0:
-                t["pr", m] = b6.tile([P, NI, COLS], F32, tag="b6", name="pr", align_bytes=64)
+                t["pr", m] = b6.tile([P, B, NI, NJ], F32, tag="b6", name="pr", align_bytes=64)
             on = nc.gpsimd if eng == "G" else nc.vector
-            on.tensor_tensor(out=t["pr", m][:, i, :], in0=t["z", m][:, i, :],
-                             in1=t["vi", i, m // 4][:, m % 4, :], op=ALU.mult)
+            on.tensor_tensor(out=t["pr", m][:, :, i, :], in0=t["z", m][:, :, i, :],
+                             in1=t["vi", i, m // 4][:, m % 4, :].rearrange("p (b j) -> p b j", j=NJ), op=ALU.mult)
 
         def over_s(dst, src):
-            nc.vector.tensor_reduce(out=dst, in_=src.rearrange("p i (b j) -> p b i j", j=NJ), axis=AX.XY, op=ALU.add)
+            nc.vector.tensor_reduce(out=dst, in_=src.rearrange("p b i j -> p b (i j)"), axis=AX.X, op=ALU.add)
 
         def den(m):
             if m % 2 == 0:

@@ -19,15 +19,15 @@ FLOPS = 2 * B * S * HID * C + 2 * B * S * HID * HID + 2 * B * HID * HID
 NI, NJ = 3, 4
 COLS = B * NJ
 EARLY = 3
-VSET = (0, 1, 2)
+VSET = (2, 3, 4, 5)
 HEAD = (("l1", 0), ("x", 0), ("x", 1), ("l1", 1), ("x", 2), ("x", 3), ("l1", 2))
 FILL_AT = 3
-HALF, L3_AT, MEAN_AT, UEV_AT, UT_AT, REP_AT = 1, 5, 8, 8, 16, 17
-W_AT = (15, 15, 15, 15, 17, 19, 21, 23)
-LAG_Q, LAG_CAST, LAG_QV, LAG_EXP, LAG_DEN, LAG_NUM, LAG_FIN = 3, 1, 2, 2, 1, 4, 4
-CAST_ON = "VVVVVV"
+HALF, L3_AT, MEAN_AT, UEV_AT, UT_AT, REP_AT = 2, 1, 5, 6, 15, 16
+W_AT = (14, 15, 15, 15, 17, 19, 21, 23)
+LAG_Q, LAG_CAST, LAG_QV, LAG_EXP, LAG_DEN, LAG_NUM, LAG_FIN = 3, 3, 1, 2, 1, 4, 4
+CAST_ON = "VSVVVV"
 X_ON = "SVSVSS"
-L1_ON = "VSSS"
+L1_ON = "SVSV"
 W_ON = "SS"
 
 
@@ -48,14 +48,12 @@ def tile_attentionmechanism_pa_kernel(tc, v_i, v_q, l1_w, l1_b, w_vi0, w_u0, b_u
         ident_b = const.tile([P, P], BF16, name="ident_b")
         masks.make_identity(nc, ident_b[:])
 
-        lb_raw = const.tile([P, 8], BF16, name="lb_raw")
-        bu_raw = const.tile([P, 8], BF16, name="bu_raw")
-        nc.scalar.dma_start(out=lb_raw[:].rearrange("p (a e) -> p a e", e=2),
-                            in_=l1_b.rearrange("(a p e) -> p a e", p=P, e=2))
-        nc.scalar.dma_start(out=bu_raw[:].rearrange("p (a e) -> p a e", e=2),
-                            in_=b_u0.rearrange("(a p e) -> p a e", p=P, e=2))
-        lb = const.tile([P, 8], F32, name="lb")
-        bu = const.tile([P, 8], F32, name="bu")
+        b_rows = const.tile([P, P], F32, name="b_rows")
+        nc.gpsimd.memset(b_rows[:], 0.0)
+        nc.gpsimd.dma_start(out=b_rows[0:4, :].bitcast(BF16), in_=l1_b.rearrange("(a c) -> a c", a=4))
+        nc.gpsimd.dma_start(out=b_rows[4:8, :].bitcast(BF16), in_=b_u0.rearrange("(a c) -> a c", a=4))
+        bias = const.tile([P, 16], F32, name="bias")
+        lb, bu = bias[:, 0:8], bias[:, 8:16]
 
         words = {"l1": const.tile([P, 4, HID], U32, name="l1w", align_bytes=64),
                  "wv": const.tile([P, 2, HID], U32, name="wvw", align_bytes=64),
@@ -186,15 +184,27 @@ def tile_attentionmechanism_pa_kernel(tc, v_i, v_q, l1_w, l1_b, w_vi0, w_u0, b_u
                                      rhs=t["vq", k][:, tt - 3 * k, 512 * hf:512 * hf + 512],
                                      start=(tt == pe_steps[0]), stop=(tt == pe_steps[-1]))
 
-        def add_step(k, i):
-            first = t["vq", k][:, 0, :] if (k, i) == (VSET[0], 1) else u_sb[:]
-            nc.vector.tensor_tensor(out=u_sb[:], in0=first, in1=t["vq", k][:, i, :], op=ALU.add)
+        sums = (u_sb[:], res[:].rearrange("p m b -> p (m b)"))
 
-        def meanv(k):
-            for i in range(1 if k == VSET[0] else 0, min(3, T - 3 * k)):
-                fill.append(lambda i=i: add_step(k, i))
-            if k == VSET[-1]:
-                fill.append(lambda: nc.vector.tensor_scalar_mul(out=u_sb[:], in0=u_sb[:], scalar1=1.0 / T))
+        def add_step(n):
+            k, i = v_steps[n]
+            into = sums[n % 2]
+            if n < 2:
+                k2, i2 = v_steps[n + 2]
+                first = t["vq", k2][:, i2, :]
+            else:
+                first = into
+            nc.vector.tensor_tensor(out=into, in0=first, in1=t["vq", k][:, i, :], op=ALU.add)
+
+        v_steps = [(k, i) for k in VSET for i in range(min(3, T - 3 * k))]
+
+        def meanv():
+            for n in range(len(v_steps)):
+                if n not in (2, 3):
+                    fill.append(lambda n=n: add_step(n))
+            fill.append(lambda: nc.vector.tensor_scalar_mul(out=u_sb[:], in0=u_sb[:], scalar1=1.0 / T))
+            fill.append(lambda: nc.vector.scalar_tensor_tensor(out=u_sb[:], in0=sums[1], scalar=1.0 / T, in1=u_sb[:],
+                                                               op0=ALU.mult, op1=ALU.add))
 
         def uev():
             while fill:
@@ -322,8 +332,6 @@ def tile_attentionmechanism_pa_kernel(tc, v_i, v_q, l1_w, l1_b, w_vi0, w_u0, b_u
             ld("wu", k)
         for k in range(4):
             ld("wv", k)
-        nc.vector.tensor_copy(out=lb[:], in_=lb_raw[:])
-        nc.vector.tensor_copy(out=bu[:], in_=bu_raw[:])
 
         def x_bank(g, k):
             tx(g, k)
@@ -373,6 +381,10 @@ def tile_attentionmechanism_pa_kernel(tc, v_i, v_q, l1_w, l1_b, w_vi0, w_u0, b_u
                 continue
             for k in range(6):
                 x_bank(g, k)
+                if (g, k) == (3, 1):
+                    b_bank = psum.tile([P, P], F32, tag="ps", name="b_bank")
+                    nc.tensor.transpose(b_bank[:], b_rows[:], ident_f[:])
+                    nc.vector.tensor_copy(out=bias[:], in_=b_bank[:, 0:8].bitcast(BF16))
             if g >= 1:
                 for i, m in early:
                     m1(i, m, g - 1)
@@ -380,8 +392,7 @@ def tile_attentionmechanism_pa_kernel(tc, v_i, v_q, l1_w, l1_b, w_vi0, w_u0, b_u
         for n, (i, m) in enumerate(units):
             unit1(i, m)
             if n == FILL_AT:
-                for k in VSET:
-                    meanv(k)
+                meanv()
             if n == L3_AT:
                 for g in range(4):
                     w_bank("l1", 3, g, L1_ON[g])

@@ -22,11 +22,12 @@ EARLY = 3
 VSET = (2, 3, 4, 5)
 HEAD = (("l1", 0), ("x", 0), ("x", 1), ("l1", 1), ("x", 2), ("x", 3), ("l1", 2))
 FILL_AT = 3
-HALF, L3_AT, MEAN_AT, UEV_AT, UT_AT, REP_AT = 2, 1, 5, 6, 15, 16
-W_AT = (14, 15, 15, 15, 17, 19, 21, 23)
-LAG_Q, LAG_CAST, LAG_QV, LAG_EXP, LAG_DEN, LAG_NUM, LAG_FIN = 3, 3, 1, 2, 1, 4, 4
+HALF, L3_AT, MEAN_AT, UEV_AT, UT_AT, REP_AT = 2, 0, 8, 8, 16, 18
+W_AT = (11, 11, 15, 15, 19, 19, 23, 23)
+LAG_Q, LAG_CAST, LAG_QV, LAG_EXP, LAG_DEN, LAG_NUM, LAG_FIN = 3, 3, 1, 2, 2, 6, 11
 CAST_ON = "VSVVVV"
 X_ON = "SVSVSS"
+L1_LATE_ON = "VSSS"
 L1_ON = "SVSV"
 W_ON = "SS"
 
@@ -286,8 +287,8 @@ def tile_attentionmechanism_pa_kernel(tc, v_i, v_q, l1_w, l1_b, w_vi0, w_u0, b_u
 
         def quot(m):
             if m % 2 == 1:
-                nc.vector.tensor_tensor(out=res[:, m - 1:m + 1, :], in0=t["num", m // 2][:], in1=t["den", m // 2][:],
-                                        op=ALU.mult)
+                on = nc.vector if m == 7 else nc.gpsimd
+                on.tensor_tensor(out=res[:, m - 1:m + 1, :], in0=t["num", m // 2][:], in1=t["den", m // 2][:], op=ALU.mult)
 
         def final(k):
             fin = psum.tile([P, 2, P], F32, tag="ps", name="fin")
@@ -365,7 +366,7 @@ def tile_attentionmechanism_pa_kernel(tc, v_i, v_q, l1_w, l1_b, w_vi0, w_u0, b_u
             m2(i, m)
             th2(i, m)
             later(LAG_EXP, lambda: te(m, i, i + 1))
-            later(LAG_EXP, lambda: prod(i, m, "G"))
+            later(LAG_EXP, lambda: prod(i, m, "V" if m == 0 else "G"))
             if i == 2:
                 later(LAG_EXP + LAG_DEN, lambda: den(m))
                 later(LAG_EXP + LAG_NUM, lambda: num(m))
@@ -377,7 +378,7 @@ def tile_attentionmechanism_pa_kernel(tc, v_i, v_q, l1_w, l1_b, w_vi0, w_u0, b_u
         for what, g in HEAD:
             if what == "l1":
                 for k in range(4):
-                    w_bank("l1", g, k, L1_ON[k])
+                    w_bank("l1", g, k, (L1_LATE_ON if g == 2 else L1_ON)[k])
                 continue
             for k in range(6):
                 x_bank(g, k)
@@ -395,7 +396,7 @@ def tile_attentionmechanism_pa_kernel(tc, v_i, v_q, l1_w, l1_b, w_vi0, w_u0, b_u
                 meanv()
             if n == L3_AT:
                 for g in range(4):
-                    w_bank("l1", 3, g, L1_ON[g])
+                    w_bank("l1", 3, g, L1_LATE_ON[g])
             if n == MEAN_AT:
                 for k in range(7):
                     if k not in VSET:

@@ -22,9 +22,10 @@ EARLY = 3
 VSET = (2, 3, 4, 5)
 HEAD = (("l1", 0), ("x", 0), ("x", 1), ("l1", 1), ("x", 2), ("x", 3), ("l1", 2))
 FILL_AT = 3
+PE_DEN = (6, 7)
 HALF, L3_AT, MEAN_AT, UEV_AT, UT_AT, REP_AT = 2, 0, 8, 8, 16, 18
 W_AT = (11, 11, 15, 15, 19, 19, 23, 23)
-LAG_Q, LAG_CAST, LAG_QV, LAG_EXP, LAG_DEN, LAG_NUM, LAG_FIN = 3, 3, 1, 2, 2, 6, 11
+LAG_Q, LAG_CAST, LAG_QV, LAG_EXP, LAG_DEN, LAG_NUM, LAG_FIN = 3, 3, 1, 2, 4, 7, 8
 CAST_ON = "VSVVVV"
 X_ON = "SVSVSS"
 L1_LATE_ON = "VSSS"
@@ -253,35 +254,44 @@ def tile_attentionmechanism_pa_kernel(tc, v_i, v_q, l1_w, l1_b, w_vi0, w_u0, b_u
 
         def th2(i, m):
             if i == 0 and m == 0:
-                t["zs"] = big.tile([P, 4, B, NI, NJ], F32, tag="big", name="zs", align_bytes=64)
+                t["zs"] = big.tile([P, 4, NI, COLS], F32, tag="big", name="zs", align_bytes=64)
             if i == 0:
                 t["z", m] = t["zs"][:, m % 4]
-            nc.scalar.activation(out=t["z", m][:, :, i, :], in_=t["p2", i, m][:].rearrange("p (b j) -> p b j", j=NJ),
-                                 func=ACT.Tanh, bias=bu[:, m:m + 1], scale=1.0)
+            nc.scalar.activation(out=t["z", m][:, i, :], in_=t["p2", i, m][:], func=ACT.Tanh, bias=bu[:, m:m + 1], scale=1.0)
 
         def te(m, i0, i1):
-            nc.scalar.activation(out=t["z", m][:, :, i0:i1, :], in_=t["z", m][:, :, i0:i1, :], func=ACT.Exp)
+            nc.scalar.activation(out=t["z", m][:, i0:i1, :], in_=t["z", m][:, i0:i1, :], func=ACT.Exp)
 
         def prod(i, m, eng):
             if i == 0:
-                t["pr", m] = b6.tile([P, B, NI, NJ], F32, tag="b6", name="pr", align_bytes=64)
+                t["pr", m] = b6.tile([P, NI, COLS], F32, tag="b6", name="pr", align_bytes=64)
             on = nc.gpsimd if eng == "G" else nc.vector
-            on.tensor_tensor(out=t["pr", m][:, :, i, :], in0=t["z", m][:, :, i, :],
-                             in1=t["vi", i, m // 4][:, m % 4, :].rearrange("p (b j) -> p b j", j=NJ), op=ALU.mult)
+            on.tensor_tensor(out=t["pr", m][:, i, :], in0=t["z", m][:, i, :], in1=t["vi", i, m // 4][:, m % 4, :], op=ALU.mult)
 
         def over_s(dst, src):
-            nc.vector.tensor_reduce(out=dst, in_=src.rearrange("p b i j -> p b (i j)"), axis=AX.X, op=ALU.add)
+            nc.vector.tensor_reduce(out=dst, in_=src.rearrange("p i (b j) -> p b i j", j=NJ), axis=AX.XY, op=ALU.add)
 
         def den(m):
             if m % 2 == 0:
                 t["den", m // 2] = small.tile([P, 2, B], F32, tag="den", name="den")
-            over_s(t["den", m // 2][:, m % 2, :], t["z", m])
+            if m in PE_DEN:
+                bank = psum.tile([P, COLS], F32, tag="ps", name="den_bank")
+                for i in range(NI):
+                    nc.tensor.matmul(out=bank[:], lhsT=ident_f[:], rhs=t["z", m][:, i, :], start=(i == 0),
+                                     stop=(i == NI - 1))
+                t["den_bank", m] = bank
+            else:
+                over_s(t["den", m // 2][:, m % 2, :], t["z", m])
 
         def num(m):
             if m % 2 == 0:
                 t["num", m // 2] = small.tile([P, 2, B], F32, tag="num", name="num")
             else:
                 d = t["den", m // 2]
+                for k in (m - 1, m):
+                    if k in PE_DEN:
+                        nc.vector.tensor_reduce(out=d[:, k % 2, :], in_=t["den_bank", k][:].rearrange("p (b j) -> p b j", j=NJ),
+                                                axis=AX.X, op=ALU.add)
                 nc.vector.reciprocal(out=d[:], in_=d[:])
             over_s(t["num", m // 2][:, m % 2, :], t["pr", m][:])
 

from contextlib import ExitStack

import concourse.masks as masks
import concourse.mybir as mybir

F32 = mybir.dt.float32
BF16 = mybir.dt.bfloat16
U32 = mybir.dt.uint32
U8 = mybir.dt.uint8
FP8X4 = mybir.dt.float8_e4m3fn_x4
ACT = mybir.ActivationFunctionType
ALU = mybir.AluOpType
AX = mybir.AxisListType

P = 128
B, C, S, T, HID = 128, 2048, 12, 20, 1024
FLOPS = 2 * B * S * HID * C + 2 * B * S * HID * HID + 2 * B * HID * HID

NI, NJ = 3, 4
COLS = B * NJ
EARLY = 3
VSET = (2, 3, 4, 5)
HEAD = (("l1", 0), ("x", 0), ("x", 1), ("l1", 1), ("x", 2), ("x", 3), ("l1", 2))
FILL_AT = 3
PE_DEN = (6, 7)
HALF, L3_AT, MEAN_AT, UEV_AT, UT_AT, REP_AT = 2, 0, 8, 8, 16, 18
W_AT = (11, 11, 15, 15, 19, 19, 23, 23)
LAG_Q, LAG_CAST, LAG_QV, LAG_EXP, LAG_DEN, LAG_NUM, LAG_FIN = 3, 3, 1, 2, 4, 7, 8
CAST_ON = "VSVVVV"
X_ON = "SVSVSS"
L1_LATE_ON = "VSSS"
L1_ON = "SVSV"
W_ON = "SS"


def tile_attentionmechanism_pa_kernel(tc, v_i, v_q, l1_w, l1_b, w_vi0, w_u0, b_u0, out):
    nc = tc.nc
    with ExitStack() as ctx:
        const = ctx.enter_context(tc.tile_pool(name="const", bufs=1))
        k8 = ctx.enter_context(tc.tile_pool(name="k8", bufs=6))
        b6 = ctx.enter_context(tc.tile_pool(name="b6", bufs=8))
        k12 = ctx.enter_context(tc.tile_pool(name="k12", bufs=2))
        gwp = ctx.enter_context(tc.tile_pool(name="gwp", bufs=2))
        big = ctx.enter_context(tc.tile_pool(name="big", bufs=1))
        small = ctx.enter_context(tc.tile_pool(name="small", bufs=2))
        psum = ctx.enter_context(tc.psum_pool(name="psum", bufs=8))

        ident_f = const.tile([P, P], F32, name="ident_f")
        masks.make_identity(nc, ident_f[:])
        ident_b = const.tile([P, P], BF16, name="ident_b")
        masks.make_identity(nc, ident_b[:])

        b_rows = const.tile([P, P], F32, name="b_rows")
        nc.gpsimd.memset(b_rows[:], 0.0)
        nc.gpsimd.dma_start(out=b_rows[0:4, :].bitcast(BF16), in_=l1_b.rearrange("(a c) -> a c", a=4))
        nc.gpsimd.dma_start(out=b_rows[4:8, :].bitcast(BF16), in_=b_u0.rearrange("(a c) -> a c", a=4))
        bias = const.tile([P, 16], F32, name="bias")
        lb, bu = bias[:, 0:8], bias[:, 8:16]

        words = {"l1": const.tile([P, 4, HID], U32, name="l1w", align_bytes=64),
                 "wv": const.tile([P, 2, HID], U32, name="wvw", align_bytes=64),
                 "wu": const.tile([P, 2, HID], U32, name="wuw", align_bytes=64)}
        planes = {"l1": const.tile([P, 4, HID], U8, name="l1s", align_bytes=64),
                  "wv": const.tile([P, 2, HID], U8, name="wvs", align_bytes=64),
                  "wu": const.tile([P, 2, HID], U8, name="wus", align_bytes=64)}
        xw = big.tile([P, 4, NI * COLS], U32, tag="big", name="xw", align_bytes=64)
        xs = const.tile([P, 4, NI * COLS], U8, name="xs", align_bytes=64)
        viw = const.tile([P, 2, NI * COLS], U32, name="viw", align_bytes=64)
        vis = const.tile([P, 2, NI * COLS], U8, name="vis", align_bytes=64)
        urw = const.tile([P, 2, COLS], U32, name="urw", align_bytes=64)
        urs = const.tile([P, 2, COLS], U8, name="urs", align_bytes=64)
        u_sb = const.tile([P, HID], F32, name="u_sb")
        res = const.tile([P, 8, B], F32, name="res")
        gu = const.tile([P, 2, B, 4], BF16, name="gu", align_bytes=64)

        t = {}

        l1_rows = l1_w.rearrange("(a p e) c -> a p e c", p=P, e=2)
        x_flat = v_i.rearrange("b c h w -> b (c h w)")
        w_rows = {"wu": w_u0.rearrange("(a p e) c -> a p e c", p=P, e=2),
                  "wv": w_vi0.rearrange("(a p e) c -> a p e c", p=P, e=2)}

        def ld(what, i):
            if what == "l1":
                t["l1", i] = k8.tile([P, 2, C], BF16, tag="k8", name="l1sb", align_bytes=64)
                n = C // 4 if i == 0 else C
                for c0 in range(0, C, n):
                    nc.sync.dma_start(out=t["l1", i][:, :, c0:c0 + n], in_=l1_rows[i][:, :, c0:c0 + n])
            elif what == "x":
                t["x", i] = b6.tile([P, 256 * S], BF16, tag="b6", name="xq", align_bytes=64)
                nc.sync.dma_start(out=t["x", i][:], in_=x_flat[:, 256 * S * i:256 * S * (i + 1)])
            elif what == "vq":
                nt = min(3, T - 3 * i)
                t["vq", i] = b6.tile([P, 3, HID], BF16, tag="b6", name="vq", align_bytes=64)
                nc.sync.dma_start(out=t["vq", i][:, 0:nt, :], in_=v_q[:, 3 * i:3 * i + nt, :])
            else:
                t[what, i] = b6.tile([P, 2, HID], BF16, tag="b6", name="wsb", align_bytes=64)
                nc.sync.dma_start(out=t[what, i][:], in_=w_rows[what][i])

        def rows_of(w, a, e):
            return t[w, a][:, e, :]

        def copy_on(eng, dst, src):
            if eng == "V":
                nc.vector.tensor_copy(out=dst, in_=src)
            else:
                nc.scalar.copy(out=dst, in_=src)

        def tw(w, a, g):
            bank = psum.tile([P, 2, 2, P], F32, tag="ps", name="wbank")
            t["wb", w, a, g] = bank
            for u in range(2):
                for e in range(2):
                    nc.tensor.transpose(
                        bank[:, u, e, :],
                        rows_of(w, a, e).bitcast(F32)[:, 256 * g + 128 * u:256 * g + 128 * u + 128],
                        ident_f[:])

        def ew(w, a, g, eng):
            gw = gwp.tile([P, 1024], BF16, tag="gw" + eng, bufs=2 if eng == "V" else 3, name="gw", align_bytes=64)
            t["gw", w, a, g] = gw
            copy_on(eng, gw[:].bitcast(F32).rearrange("p (c u) -> p c u", u=2),
                    t["wb", w, a, g][:].rearrange("p u e h -> p (e h) u"))

        def qw(w, a, g):
            nc.vector.quantize_mx(out=words[w][:, g, 256 * a:256 * a + 256].bitcast(FP8X4),
                                  scales=planes[w][:, g, 256 * a:256 * a + 256],
                                  in_=t["gw", w, a, g][:])

        def tx(g, k):
            bank = psum.tile([P, 4, P], F32, tag="ps", name="xbank")
            t["xb", g, k] = bank
            for u in range(2):
                xv = t["x", 2 * g + u][:].bitcast(F32).rearrange("b (p e k) -> b e k p", p=P, e=2, k=6)
                for e in range(2):
                    nc.tensor.transpose(bank[:, 2 * u + e, :], xv[:, e, k, :], ident_f[:])

        def ex(g, k, eng):
            if k == 0:
                t["gx", g] = k12.tile([P, NI * COLS * 4], BF16, tag="k12", name="gx", align_bytes=64)
            gxv = t["gx", g][:].rearrange("p (i b k r t) -> p i k b r t", i=NI, b=B, k=2, r=2, t=4)
            copy_on(eng, gxv[:, k // 2, k % 2], t["xb", g, k][:].bitcast(BF16).rearrange("p t (b r) -> p b r t", r=2))

        def qx(g, i):
            nc.vector.quantize_mx(out=xw[:, g, COLS * i:COLS * i + COLS].bitcast(FP8X4),
                                  scales=xs[:, g, COLS * i:COLS * i + COLS],
                                  in_=t["gx", g][:, 4 * COLS * i:4 * COLS * (i + 1)])

        def m1(i, m, g):
            if g == 0:
                t["p1", i, m] = psum.tile([P, COLS], F32, tag="ps", name="ps1")
            nc.tensor.matmul_mx(
                out=t["p1", i, m][:],
                lhsT=words["l1"][:, g, P * m:P * m + P].bitcast(FP8X4),
                lhsT_scale=planes["l1"][:, g, P * m:P * m + P],
                rhs=xw[:, g, COLS * i:COLS * i + COLS].bitcast(FP8X4),
                rhs_scale=xs[:, g, COLS * i:COLS * i + COLS],
                start=(g == 0), stop=(g == 3))

        def th1(i, m):
            if m % 4 == 0:
                t["vi", i, m // 4] = k8.tile([P, 4, COLS], F32, tag="k8", name="vi", align_bytes=64)
            nc.scalar.activation(out=t["vi", i, m // 4][:, m % 4, :], in_=t["p1", i, m][:], func=ACT.Tanh,
                                 bias=lb[:, m:m + 1], scale=1.0)

        def cast(i, gp, h, eng):
            if i == 0 and h == 0:
                t["gv", gp] = k12.tile([P, NI, COLS * 4], BF16, tag="k12", name="gv", align_bytes=64)
            n = COLS // 2
            copy_on(eng, t["gv", gp][:, i, 4 * n * h:4 * n * (h + 1)].rearrange("p (c t) -> p c t", t=4),
                    t["vi", i, gp][:, :, n * h:n * h + n].rearrange("p t c -> p c t"))

        def qv(i, gp):
            nc.vector.quantize_mx(out=viw[:, gp, COLS * i:COLS * i + COLS].bitcast(FP8X4),
                                  scales=vis[:, gp, COLS * i:COLS * i + COLS],
                                  in_=t["gv", gp][:, i, :])

        pe_steps = [tt for tt in range(T) if tt // 3 not in VSET]

        def meanp(k):
            for tt in range(3 * k, min(3 * k + 3, T)):
                for hf in range(2):
                    if tt == pe_steps[0]:
                        t["ups", hf] = psum.tile([P, 512], F32, tag="ps", name="u_ps")
                    nc.tensor.matmul(out=t["ups", hf][:], lhsT=ident_b[:],
                                     rhs=t["vq", k][:, tt - 3 * k, 512 * hf:512 * hf + 512],
                                     start=(tt == pe_steps[0]), stop=(tt == pe_steps[-1]))

        sums = (u_sb[:], res[:].rearrange("p m b -> p (m b)"))

        def add_step(n):
            k, i = v_steps[n]
            into = sums[n % 2]
            if n < 2:
                k2, i2 = v_steps[n + 2]
                first = t["vq", k2][:, i2, :]
            else:
                first = into
            nc.vector.tensor_tensor(out=into, in0=first, in1=t["vq", k][:, i, :], op=ALU.add)

        v_steps = [(k, i) for k in VSET for i in range(min(3, T - 3 * k))]

        def meanv():
            for n in range(len(v_steps)):
                if n not in (2, 3):
                    fill.append(lambda n=n: add_step(n))
            fill.append(lambda: nc.vector.tensor_scalar_mul(out=u_sb[:], in0=u_sb[:], scalar1=1.0 / T))
            fill.append(lambda: nc.vector.scalar_tensor_tensor(out=u_sb[:], in0=sums[1], scalar=1.0 / T, in1=u_sb[:],
                                                               op0=ALU.mult, op1=ALU.add))

        def uev():
            while fill:
                fill_one()
            if not pe_steps:
                return
            for hf in range(2):
                cols = slice(512 * hf, 512 * hf + 512)
                nc.vector.scalar_tensor_tensor(out=u_sb[:, cols], in0=t["ups", hf][:], scalar=1.0 / T,
                                               in1=u_sb[:, cols], op0=ALU.mult, op1=ALU.add)

        def ut(gp):
            bank = psum.tile([P, 4, B], F32, tag="ps", name="ubank")
            t["ub", gp] = bank
            u_cols = u_sb[:].rearrange("b (a p e) -> b a e p", p=P, e=2)
            for k in range(4):
                m = 4 * gp + k
                nc.tensor.transpose(bank[:, k, :], u_cols[:, m // 2, m % 2, :], ident_f[:])

        def eu(gp):
            nc.scalar.copy(out=gu[:, gp], in_=t["ub", gp][:].rearrange("p t b -> p b t"))

        def rep_u(gp):
            t["gur", gp] = b6.tile([P, B, NJ, 4], BF16, tag="b6", name="gur", align_bytes=64)
            nc.vector.tensor_copy(out=t["gur", gp][:], in_=gu[:, gp].unsqueeze(2).to_broadcast([P, B, NJ, 4]))

        def qu(gp):
            nc.vector.quantize_mx(out=urw[:, gp, :].bitcast(FP8X4), scales=urs[:, gp, :],
                                  in_=t["gur", gp][:].rearrange("p b j t -> p (b j t)"))

        def m2(i, m):
            ps = psum.tile([P, COLS], F32, tag="ps", name="ps2")
            t["p2", i, m] = ps
            cols = slice(COLS * i, COLS * i + COLS)
            for k in range(4):
                gp = k % 2
                w = "wu" if k < 2 else "wv"
                nc.tensor.matmul_mx(
                    out=ps[:],
                    lhsT=words[w][:, gp, P * m:P * m + P].bitcast(FP8X4),
                    lhsT_scale=planes[w][:, gp, P * m:P * m + P],
                    rhs=(urw[:, gp, :] if k < 2 else viw[:, gp, cols]).bitcast(FP8X4),
                    rhs_scale=urs[:, gp, :] if k < 2 else vis[:, gp, cols],
                    start=(k == 0), stop=(k == 3))

        def th2(i, m):
            if i == 0 and m == 0:
                t["zs"] = big.tile([P, 4, NI, COLS], F32, tag="big", name="zs", align_bytes=64)
            if i == 0:
                t["z", m] = t["zs"][:, m % 4]
            nc.scalar.activation(out=t["z", m][:, i, :], in_=t["p2", i, m][:], func=ACT.Tanh, bias=bu[:, m:m + 1], scale=1.0)

        def te(m, i0, i1):
            nc.scalar.activation(out=t["z", m][:, i0:i1, :], in_=t["z", m][:, i0:i1, :], func=ACT.Exp)

        def prod(i, m, eng):
            if i == 0:
                t["pr", m] = b6.tile([P, NI, COLS], F32, tag="b6", name="pr", align_bytes=64)
            on = nc.gpsimd if eng == "G" else nc.vector
            on.tensor_tensor(out=t["pr", m][:, i, :], in0=t["z", m][:, i, :], in1=t["vi", i, m // 4][:, m % 4, :], op=ALU.mult)

        def over_s(dst, src):
            nc.vector.tensor_reduce(out=dst, in_=src.rearrange("p i (b j) -> p b i j", j=NJ), axis=AX.XY, op=ALU.add)

        def den(m):
            if m % 2 == 0:
                t["den", m // 2] = small.tile([P, 2, B], F32, tag="den", name="den")
            if m in PE_DEN:
                bank = psum.tile([P, COLS], F32, tag="ps", name="den_bank")
                for i in range(NI):
                    nc.tensor.matmul(out=bank[:], lhsT=ident_f[:], rhs=t["z", m][:, i, :], start=(i == 0),
                                     stop=(i == NI - 1))
                t["den_bank", m] = bank
            else:
                over_s(t["den", m // 2][:, m % 2, :], t["z", m])

        def num(m):
            if m % 2 == 0:
                t["num", m // 2] = small.tile([P, 2, B], F32, tag="num", name="num")
            else:
                d = t["den", m // 2]
                for k in (m - 1, m):
                    if k in PE_DEN:
                        nc.vector.tensor_reduce(out=d[:, k % 2, :], in_=t["den_bank", k][:].rearrange("p (b j) -> p b j", j=NJ),
                                                axis=AX.X, op=ALU.add)
                nc.vector.reciprocal(out=d[:], in_=d[:])
            over_s(t["num", m // 2][:, m % 2, :], t["pr", m][:])

        def quot(m):
            if m % 2 == 1:
                on = nc.vector if m == 7 else nc.gpsimd
                on.tensor_tensor(out=res[:, m - 1:m + 1, :], in0=t["num", m // 2][:], in1=t["den", m // 2][:], op=ALU.mult)

        def final(k):
            fin = psum.tile([P, 2, P], F32, tag="ps", name="fin")
            for e in range(2):
                nc.tensor.transpose(fin[:, e, :], res[:, 2 * k + e, :], ident_f[:])
            cols = u_sb[:, 256 * k:256 * k + 256]
            nc.vector.tensor_tensor(out=cols.rearrange("b (p e) -> b p e", e=2),
                                    in0=fin[:].rearrange("b e p -> b p e"),
                                    in1=cols.rearrange("b (p e) -> b p e", e=2), op=ALU.add)
            nc.sync.dma_start(out=out[:, 256 * k:256 * k + 256], in_=cols)


        waiting = []
        step = [0]

        def later(lag, call):
            waiting.append((step[0] + lag, call))

        def tick():
            step[0] += 1
            due = [item for item in waiting if item[0] <= step[0]]
            waiting[:] = [item for item in waiting if item[0] > step[0]]
            for item in due:
                item[1]()

        fill = []

        def fill_one():
            if fill:
                fill.pop(0)()

        ctx.enter_context(tc.manual_schedule())
        for what, k in HEAD + (("l1", 3),):
            if what == "x":
                ld("x", 2 * k)
                ld("x", 2 * k + 1)
            else:
                ld("l1", k)
        for k in range(7):
            ld("vq", k)
        for k in range(4):
            ld("wu", k)
        for k in range(4):
            ld("wv", k)

        def x_bank(g, k):
            tx(g, k)
            ex(g, k, X_ON[k])
            if k % 2 == 1:
                later(LAG_Q, lambda: qx(g, k // 2))
            tick()

        def w_bank(w, a, g, on):
            tw(w, a, g)
            ew(w, a, g, on)
            later(LAG_Q, lambda: qw(w, a, g))
            tick()

        units = [(i, m) for m in range(4) for i in range(NI)] + [(i, m) for i in range(NI) for m in range(4, 8)]
        early = units[:EARLY]

        def unit1(i, m):
            for g in range(3 if (i, m) in early else 0, 4):
                m1(i, m, g)
            th1(i, m)
            if m % 4 == 3:
                gp = m // 4
                for h in range(2):
                    later(LAG_CAST + h * HALF, lambda h=h: cast(i, gp, h, CAST_ON[3 * gp + i]))
                later(LAG_CAST + HALF + LAG_QV, lambda: qv(i, gp))
            fill_one()
            tick()

        def unit2(i, m):
            m2(i, m)
            th2(i, m)
            later(LAG_EXP, lambda: te(m, i, i + 1))
            later(LAG_EXP, lambda: prod(i, m, "V" if m == 0 else "G"))
            if i == 2:
                later(LAG_EXP + LAG_DEN, lambda: den(m))
                later(LAG_EXP + LAG_NUM, lambda: num(m))
                later(LAG_EXP + LAG_NUM + 1, lambda: quot(m))
                if m % 2 == 1:
                    later(LAG_EXP + LAG_NUM + LAG_FIN, lambda: final(m // 2))
            tick()

        for what, g in HEAD:
            if what == "l1":
                for k in range(4):
                    w_bank("l1", g, k, (L1_LATE_ON if g == 2 else L1_ON)[k])
                continue
            for k in range(6):
                x_bank(g, k)
                if (g, k) == (3, 1):
                    b_bank = psum.tile([P, P], F32, tag="ps", name="b_bank")
                    nc.tensor.transpose(b_bank[:], b_rows[:], ident_f[:])
                    nc.vector.tensor_copy(out=bias[:], in_=b_bank[:, 0:8].bitcast(BF16))
            if g >= 1:
                for i, m in early:
                    m1(i, m, g - 1)
        w_groups = [(w, a) for w in ("wu", "wv") for a in range(4)]
        for n, (i, m) in enumerate(units):
            unit1(i, m)
            if n == FILL_AT:
                meanv()
            if n == L3_AT:
                for g in range(4):
                    w_bank("l1", 3, g, L1_LATE_ON[g])
            if n == MEAN_AT:
                for k in range(7):
                    if k not in VSET:
                        meanp(k)
            if n == UEV_AT:
                uev()
            if n == UT_AT:
                for gp in range(2):
                    ut(gp)
                    eu(gp)
            if n == REP_AT:
                for gp in range(2):
                    rep_u(gp)
                    qu(gp)
            for k in range(W_AT.count(n)):
                w, a = w_groups.pop(0)
                for g in range(2):
                    w_bank(w, a, g, W_ON[g])
        while [item for item in waiting]:
            tick()
        for m in range(8):
            for i in range(NI):
                unit2(i, m)
        while waiting:
            tick()
